import numpy as np
import ml_dtypes


def mxq(x, axis, fmt="e4m3"):
    dtype, down = {"e4m3": (ml_dtypes.float8_e4m3fn, 7), "e5m2": (ml_dtypes.float8_e5m2, 14)}[fmt]
    v = np.moveaxis(np.asarray(x, np.float32).astype(ml_dtypes.bfloat16).astype(np.float64), axis, -1)
    blocks = v.reshape(v.shape[:-1] + (-1, 32))
    amax = np.abs(blocks).max(-1, keepdims=True)
    byte = np.maximum(np.where(amax > 0, np.frexp(amax)[1] - 1 + 127, 0) - down, 1)
    scale = np.exp2(byte - 127.0)
    codes = (blocks / scale).astype(np.float32).astype(dtype).astype(np.float64)
    return np.moveaxis((codes * scale).reshape(v.shape), -1, axis)


WIDE = False


def mx_kscale(k):
    if not WIDE:
        return np.ones(k)
    levels = np.array([10, -10, 5, -5, 0])
    a = np.random.permutation(np.resize(levels, k // 512 * 4)).reshape(k // 512, 4)
    idx = np.arange(k)
    return np.exp2(a[idx // 512, idx % 128 // 32])


BF16 = ml_dtypes.bfloat16


def bf(x):
    return np.asarray(x, np.float32).astype(BF16)


def f64(x):
    return np.asarray(x).astype(np.float64)


E2M1 = np.array([0.0, 0.5, 1.0, 1.5, 2.0, 3.0, 4.0, 6.0, -0.0, -0.5, -1.0, -1.5, -2.0, -3.0, -4.0, -6.0])


def pack_weight(w, fmt):
    k, n = w.shape
    w = f64(bf(w)).reshape(k // 32, 32, n)
    amax = np.abs(w).max(1)
    if fmt == "e4m3":
        byte = np.frexp(amax)[1] - 1 + 127 - 7
    else:
        mant, ex = np.frexp(amax / 6.0)
        byte = np.where(mant > 0.5, ex, ex - 1) + 127
    byte = np.clip(np.where(amax > 0, byte, 1), 1, 254)
    scaled = (w * np.exp2(127.0 - byte)[:, None, :]).reshape(k, n).astype(np.float32)
    by_word = np.ascontiguousarray(scaled.reshape(k // 512, 128, 4, n).transpose(0, 1, 3, 2))
    if fmt == "e4m3":
        words = by_word.astype(ml_dtypes.float8_e4m3fn).view(np.uint8)
    else:
        c = by_word.astype(ml_dtypes.float4_e2m1fn).view(np.uint8) & 0xF
        words = c[..., 0::2] | (c[..., 1::2] << 4)
    return np.ascontiguousarray(words), np.ascontiguousarray(byte.astype(np.uint8).reshape(k // 512, 16, n))


def unpack_weight(words, scales, fmt):
    g, p, n, _ = words.shape
    if fmt == "e4m3":
        vals = np.ascontiguousarray(words).view(ml_dtypes.float8_e4m3fn).astype(np.float64)
    else:
        nib = np.empty((g, p, n, 4), np.uint8)
        nib[..., 0::2] = words & 0xF
        nib[..., 1::2] = words >> 4
        vals = E2M1[nib]
    vals = vals * np.repeat(np.exp2(scales.astype(np.float64) - 127.0), 8, axis=1)[..., None]
    return vals.transpose(0, 1, 3, 2).reshape(g * 512, n)


B, I, O, G, P = 1024, 512, 512, 5, 3
GRID_RANGE = (-1.0, 1.0)
L = G + P


def make_grid():
    h = (GRID_RANGE[1] - GRID_RANGE[0]) / G
    n = G + 2 * P + 1
    return np.linspace(GRID_RANGE[0] - P * h, GRID_RANGE[1] + P * h, n)


def b_spline(x, grid, k):
    x = x[..., None]
    g = grid[None, None, :]
    basis = ((x >= g[..., :-1]) & (x < g[..., 1:])).astype(np.float64)
    for p in range(1, k + 1):
        left_denom = g[..., p:-1] - g[..., :-(p + 1)]
        right_denom = g[..., p + 1:] - g[..., 1:-p]
        left_denom = np.where(left_denom > 0, left_denom, np.ones_like(left_denom))
        right_denom = np.where(right_denom > 0, right_denom, np.ones_like(right_denom))
        left = (x - g[..., :-(p + 1)]) / left_denom * basis[..., :-1]
        right = (g[..., p + 1:] - x) / right_denom * basis[..., 1:]
        basis = left + right
    return basis


def setup_inputs():
    s = mx_kscale(I)
    s = s / s.max()
    x = bf(np.random.uniform(-1.0, 1.0, (B, I)) * s)
    base_weight = np.random.uniform(-1.0, 1.0, (O, I)) * 3.0 / np.sqrt(I) / s
    base_weight_words, base_weight_scales = pack_weight(np.ascontiguousarray(base_weight.T), "e4m3")
    spline_weight = bf(np.random.standard_normal((O, I, L)) * 1.5 / np.sqrt(I))
    return {"x": x,
            "base_weight_words": base_weight_words,
            "base_weight_scales": base_weight_scales,
            "spline_weight": spline_weight}


def reference(x, base_weight_words, base_weight_scales, spline_weight):
    x = f64(x)
    grid = make_grid()
    scale_base, scale_spline = 1.0, 1.0
    base_out = mxq(x, 1, "e4m3") @ unpack_weight(base_weight_words, base_weight_scales, "e4m3")
    basis = b_spline(x, grid, P)
    spline_out = mxq(basis.reshape(B, I * L), 1, "e4m3") @ mxq(f64(spline_weight).reshape(O, I * L), 1, "e4m3").T
    return scale_base * base_out + scale_spline * spline_out

@@ -1,0 +1,171 @@
+import math
+from contextlib import ExitStack
+
+import concourse.mybir as mybir
+from concourse.masks import make_identity
+
+F32 = mybir.dt.float32
+BF16 = mybir.dt.bfloat16
+I32 = mybir.dt.int32
+U32 = mybir.dt.uint32
+U8 = mybir.dt.uint8
+FP8X4 = mybir.dt.float8_e4m3fn_x4
+ACT = mybir.ActivationFunctionType
+ALU = mybir.AluOpType
+
+P = 128
+PACK = 4
+BATCH = 1024
+FEATURES = P * PACK
+OUTS = 512
+SPLINES = 8
+FOLDS = SPLINES // 2
+ROW_TILES = BATCH // P
+OUT_TILES = OUTS // P
+TILE_COLS = P * PACK
+WORDS_PER_FEATURE = SPLINES // 2
+
+FLOPS = 2 * BATCH * OUTS * (FEATURES + FEATURES * SPLINES)
+
+
+def tile_kanlayer_kernel(tc, x, base_weight_words, base_weight_scales, spline_weight, out):
+    nc = tc.nc
+    with ExitStack() as ctx:
+        keep = ctx.enter_context(tc.tile_pool(name="keep", bufs=1))
+        weight_stage = ctx.enter_context(tc.tile_pool(name="weight_stage", bufs=2))
+        work = ctx.enter_context(tc.tile_pool(name="work", bufs=2))
+        codes = ctx.enter_context(tc.tile_pool(name="codes", bufs=3))
+        results = ctx.enter_context(tc.tile_pool(name="results", bufs=3))
+        turned = ctx.enter_context(tc.psum_pool(name="turned", bufs=4))
+        sums = ctx.enter_context(tc.psum_pool(name="sums", bufs=2))
+
+        ident = keep.tile([P, P], F32)
+        make_identity(nc, ident[:])
+        base_scales = keep.tile([P, OUTS], U8, align_bytes=64)
+        nc.vector.memset(base_scales[:].bitcast(I32), 0)
+
+        x_rows = x.rearrange("(p j) i -> p j i", j=ROW_TILES)
+        out_rows = out.rearrange("(p j) o -> p j o", j=ROW_TILES)
+        x_sb = keep.tile([P, ROW_TILES, FEATURES], BF16)
+        for j in range(0, ROW_TILES, 2):
+            nc.sync.dma_start(out=x_sb[:, j : j + 2, :], in_=x_rows[:, j : j + 2, :])
+        w_rows = spline_weight.rearrange("(c p) i l -> p c (i l)", p=P)
+        w_sb = keep.tile([P, OUT_TILES, FEATURES * SPLINES], BF16)
+        for c in range(OUT_TILES):
+            nc.sync.dma_start(out=w_sb[:, c, :], in_=w_rows[:, c, :])
+        base_codes = keep.tile([P, OUTS], U32, align_bytes=64)
+        nc.sync.dma_start(
+            out=base_codes[:].bitcast(I32),
+            in_=base_weight_words[0].rearrange("p n t -> p (n t)").bitcast(I32),
+        )
+        for quadrant in range(4):
+            nc.sync.dma_start(
+                out=base_scales[32 * quadrant : 32 * quadrant + 4, :].bitcast(I32),
+                in_=base_weight_scales[0, 4 * quadrant : 4 * quadrant + 4, :].bitcast(I32),
+            )
+
+        x_words = x_sb[:].bitcast(F32)
+        x_turned = keep.tile([P, ROW_TILES, P, PACK], BF16, align_bytes=64)
+        x_turned_words = x_turned[:].bitcast(F32)
+        for j in range(0, ROW_TILES, 2):
+            xt = turned.tile([P, 2, 2, P], F32, tag="turned")
+            for k in range(2):
+                for u in range(2):
+                    nc.tensor.transpose(xt[:, k, u, :], x_words[:, j + k, u : FEATURES // 2 : 2], ident[:])
+            nc.vector.tensor_copy(out=x_turned_words[:, j : j + 2, :, :], in_=xt[:].rearrange("p k u b -> p k b u"))
+
+        x_codes = keep.tile([P, ROW_TILES * P], U32, align_bytes=64)
+        x_scales = keep.tile([P, ROW_TILES * P], U8, align_bytes=64)
+        nc.vector.quantize_mx(
+            out=x_codes[:].bitcast(FP8X4),
+            scales=x_scales[:],
+            in_=x_turned[:].rearrange("p j b t -> p (j b t)"),
+        )
+
+        w_words = w_sb[:].bitcast(F32)
+        words_in_row = FEATURES * WORDS_PER_FEATURE
+        w_codes = keep.tile([P, SPLINES, OUTS], U32, align_bytes=64)
+        w_scales = keep.tile([P, SPLINES, OUTS], U8, align_bytes=64)
+        for w in range(WORDS_PER_FEATURE):
+            w_grouped = weight_stage.tile([P, 2, OUTS, PACK], BF16, align_bytes=64)
+            for c in range(OUT_TILES):
+                wt = turned.tile([P, PACK, P], F32, tag="turned")
+                for t in range(PACK):
+                    first_word = WORDS_PER_FEATURE * t + w
+                    nc.tensor.transpose(
+                        wt[:, t, :], w_words[:, c, first_word : words_in_row : WORDS_PER_FEATURE * PACK], ident[:]
+                    )
+                nc.scalar.copy(
+                    out=w_grouped[:, :, c * P : (c + 1) * P, :],
+                    in_=wt[:].bitcast(BF16).rearrange("p t (o e) -> p e o t", e=2),
+                )
+            nc.vector.quantize_mx(
+                out=w_codes[:, 2 * w : 2 * w + 2, :].rearrange("p l o -> p (l o)").bitcast(FP8X4),
+                scales=w_scales[:, 2 * w : 2 * w + 2, :].rearrange("p l o -> p (l o)"),
+                in_=w_grouped[:].rearrange("p e o t -> p (e o t)"),
+            )
+
+        for j in range(ROW_TILES):
+            x_tile = x_turned[:, j, :, :].rearrange("p b t -> p (b t)")
+
+            dist = work.tile([P, FOLDS, TILE_COLS], F32)
+            for r in range(FOLDS):
+                nc.scalar.activation(out=dist[:, r, :], in_=x_tile, func=ACT.Abs, scale=1.25, bias=(1.5 - r) / 2.0)
+            nc.scalar.activation(out=dist[:], in_=dist[:], func=ACT.Abs, scale=1.0, bias=-1.0)
+            neg_m = work.tile([P, FOLDS, TILE_COLS], F32)
+            nc.vector.tensor_scalar(out=neg_m[:], in0=dist[:], scalar1=1.0, scalar2=-1.0, op0=ALU.min, op1=ALU.add)
+            outer = work.tile([P, FOLDS, TILE_COLS], F32)
+            nc.scalar.activation(out=outer[:], in_=neg_m[:], func=ACT.Square, scale=math.sqrt(4.0 / 3.0))
+            inner = work.tile([P, FOLDS, TILE_COLS], F32)
+            nc.scalar.activation(out=inner[:], in_=neg_m[:], func=ACT.Square, scale=2.0, bias=2.0)
+            nc.vector.scalar_tensor_tensor(
+                out=outer[:], in0=outer[:], scalar=-1.0, in1=neg_m[:], op0=ALU.mult, op1=ALU.mult
+            )
+            nc.vector.tensor_tensor(out=inner[:], in0=inner[:], in1=neg_m[:], op=ALU.mult)
+            value = work.tile([P, FOLDS, TILE_COLS], BF16)
+            nc.vector.scalar_tensor_tensor(
+                out=value[:], in0=inner[:], scalar=2.0 / 3.0, in1=outer[:], op0=ALU.add, op1=ALU.min
+            )
+            below = work.tile([P, FOLDS, TILE_COLS], BF16)
+            for r in range(FOLDS):
+                nc.vector.tensor_scalar(
+                    out=below[:, r, :], in0=x_tile, scalar1=(r - 1.5) / 2.5, scalar2=None, op0=ALU.is_lt
+                )
+            low = work.tile([P, FOLDS, TILE_COLS], BF16, align_bytes=64)
+            nc.vector.tensor_tensor(out=low[:], in0=value[:], in1=below[:], op=ALU.mult)
+            high = work.tile([P, FOLDS, TILE_COLS], BF16, align_bytes=64)
+            nc.vector.tensor_tensor(out=high[:], in0=value[:], in1=low[:], op=ALU.subtract)
+
+            b_codes = codes.tile([P, SPLINES, P], U32, align_bytes=64)
+            b_scales = codes.tile([P, SPLINES, P], U8, align_bytes=64)
+            for half, splines in ((0, low), (1, high)):
+                l0 = half * FOLDS
+                nc.vector.quantize_mx(
+                    out=b_codes[:, l0 : l0 + FOLDS, :].rearrange("p l b -> p (l b)").bitcast(FP8X4),
+                    scales=b_scales[:, l0 : l0 + FOLDS, :].rearrange("p l b -> p (l b)"),
+                    in_=splines[:].rearrange("p r c -> p (r c)"),
+                )
+
+            acc = sums.tile([P, OUTS], F32)
+            nc.tensor.matmul_mx(
+                out=acc[:],
+                lhsT=x_codes[:, j * P : (j + 1) * P].bitcast(FP8X4),
+                lhsT_scale=x_scales[:, j * P : (j + 1) * P],
+                rhs=base_codes[:].bitcast(FP8X4),
+                rhs_scale=base_scales[:],
+                start=True,
+                stop=False,
+            )
+            for l in range(SPLINES):
+                nc.tensor.matmul_mx(
+                    out=acc[:],
+                    lhsT=b_codes[:, l, :].bitcast(FP8X4),
+                    lhsT_scale=b_scales[:, l, :],
+                    rhs=w_codes[:, l, :].bitcast(FP8X4),
+                    rhs_scale=w_scales[:, l, :],
+                    start=False,
+                    stop=(l == SPLINES - 1),
+                )
+            result = results.tile([P, OUTS], F32)
+            nc.scalar.copy(out=result[:], in_=acc[:])
+            nc.sync.dma_start(out=out_rows[:, j, :], in_=result[:])

@@ -24,6 +24,8 @@ ROW_TILES = BATCH // P
 OUT_TILES = OUTS // P
 TILE_COLS = P * PACK
 WORDS_PER_FEATURE = SPLINES // 2
+MULTIPLY_LAG = OUT_TILES - 1
+X_BOUND = 4.0
 
 FLOPS = 2 * BATCH * OUTS * (FEATURES + FEATURES * SPLINES)
 
@@ -32,12 +34,13 @@ def tile_kanlayer_kernel(tc, x, base_weight_words, base_weight_scales, spline_we
     nc = tc.nc
     with ExitStack() as ctx:
         keep = ctx.enter_context(tc.tile_pool(name="keep", bufs=1))
-        weight_stage = ctx.enter_context(tc.tile_pool(name="weight_stage", bufs=2))
+        weight_stage = ctx.enter_context(tc.tile_pool(name="weight_stage", bufs=WORDS_PER_FEATURE))
         work = ctx.enter_context(tc.tile_pool(name="work", bufs=2))
-        codes = ctx.enter_context(tc.tile_pool(name="codes", bufs=3))
+        codes = ctx.enter_context(tc.tile_pool(name="codes", bufs=MULTIPLY_LAG + 2))
         results = ctx.enter_context(tc.tile_pool(name="results", bufs=3))
-        turned = ctx.enter_context(tc.psum_pool(name="turned", bufs=4))
-        sums = ctx.enter_context(tc.psum_pool(name="sums", bufs=2))
+        turned = ctx.enter_context(tc.psum_pool(name="turned", bufs=WORDS_PER_FEATURE))
+        sums = ctx.enter_context(tc.psum_pool(name="sums", bufs=3))
+        ctx.enter_context(tc.manual_schedule())
 
         ident = keep.tile([P, P], F32)
         make_identity(nc, ident[:])
@@ -67,12 +70,21 @@ def tile_kanlayer_kernel(tc, x, base_weight_words, base_weight_scales, spline_we
         x_words = x_sb[:].bitcast(F32)
         x_turned = keep.tile([P, ROW_TILES, P, PACK], BF16, align_bytes=64)
         x_turned_words = x_turned[:].bitcast(F32)
+        x_safe = keep.tile([P, ROW_TILES, P, PACK], BF16)
         for j in range(0, ROW_TILES, 2):
             xt = turned.tile([P, 2, 2, P], F32, tag="turned")
             for k in range(2):
                 for u in range(2):
                     nc.tensor.transpose(xt[:, k, u, :], x_words[:, j + k, u : FEATURES // 2 : 2], ident[:])
             nc.vector.tensor_copy(out=x_turned_words[:, j : j + 2, :, :], in_=xt[:].rearrange("p k u b -> p k b u"))
+            nc.vector.tensor_scalar(
+                out=x_safe[:, j : j + 2, :, :],
+                in0=x_turned[:, j : j + 2, :, :],
+                scalar1=-X_BOUND,
+                scalar2=X_BOUND,
+                op0=ALU.max,
+                op1=ALU.min,
+            )
 
         x_codes = keep.tile([P, ROW_TILES * P], U32, align_bytes=64)
         x_scales = keep.tile([P, ROW_TILES * P], U8, align_bytes=64)
@@ -86,66 +98,50 @@ def tile_kanlayer_kernel(tc, x, base_weight_words, base_weight_scales, spline_we
         words_in_row = FEATURES * WORDS_PER_FEATURE
         w_codes = keep.tile([P, SPLINES, OUTS], U32, align_bytes=64)
         w_scales = keep.tile([P, SPLINES, OUTS], U8, align_bytes=64)
-        for w in range(WORDS_PER_FEATURE):
-            w_grouped = weight_stage.tile([P, 2, OUTS, PACK], BF16, align_bytes=64)
-            for c in range(OUT_TILES):
+
+        def turn_weights(c):
+            pairs = []
+            for w in range(WORDS_PER_FEATURE):
                 wt = turned.tile([P, PACK, P], F32, tag="turned")
                 for t in range(PACK):
                     first_word = WORDS_PER_FEATURE * t + w
                     nc.tensor.transpose(
                         wt[:, t, :], w_words[:, c, first_word : words_in_row : WORDS_PER_FEATURE * PACK], ident[:]
                     )
-                nc.scalar.copy(
-                    out=w_grouped[:, :, c * P : (c + 1) * P, :],
-                    in_=wt[:].bitcast(BF16).rearrange("p t (o e) -> p e o t", e=2),
-                )
-            nc.vector.quantize_mx(
-                out=w_codes[:, 2 * w : 2 * w + 2, :].rearrange("p l o -> p (l o)").bitcast(FP8X4),
-                scales=w_scales[:, 2 * w : 2 * w + 2, :].rearrange("p l o -> p (l o)"),
-                in_=w_grouped[:].rearrange("p e o t -> p (e o t)"),
-            )
+                w_grouped = weight_stage.tile([P, 2, P, PACK], BF16, align_bytes=64)
+                nc.scalar.copy(out=w_grouped[:], in_=wt[:].bitcast(BF16).rearrange("p t (o e) -> p e o t", e=2))
+                pairs.append(w_grouped)
+            return pairs
 
-        for j in range(ROW_TILES):
-            x_tile = x_turned[:, j, :, :].rearrange("p b t -> p (b t)")
+        def quantise_weights(c, pairs):
+            for w in range(WORDS_PER_FEATURE):
+                for e in range(2):
+                    nc.vector.quantize_mx(
+                        out=w_codes[:, 2 * w + e, c * P : (c + 1) * P].bitcast(FP8X4),
+                        scales=w_scales[:, 2 * w + e, c * P : (c + 1) * P],
+                        in_=pairs[w][:, e, :, :].rearrange("p o t -> p (o t)"),
+                    )
 
-            dist = work.tile([P, FOLDS, TILE_COLS], F32)
+        def scalar_stage(j):
+            x_tile = x_safe[:, j, :, :].rearrange("p b t -> p (b t)")
+            half_s = work.tile([P, FOLDS, TILE_COLS], F32)
             for r in range(FOLDS):
-                nc.scalar.activation(out=dist[:, r, :], in_=x_tile, func=ACT.Abs, scale=1.25, bias=(1.5 - r) / 2.0)
-            nc.scalar.activation(out=dist[:], in_=dist[:], func=ACT.Abs, scale=1.0, bias=-1.0)
-            neg_m = work.tile([P, FOLDS, TILE_COLS], F32)
-            nc.vector.tensor_scalar(out=neg_m[:], in0=dist[:], scalar1=1.0, scalar2=-1.0, op0=ALU.min, op1=ALU.add)
+                nc.scalar.activation(out=half_s[:, r, :], in_=x_tile, func=ACT.Abs, scale=1.25, bias=(1.5 - r) / 2.0)
+            nc.scalar.activation(out=half_s[:], in_=half_s[:], func=ACT.Abs, scale=1.0, bias=-1.0)
             outer = work.tile([P, FOLDS, TILE_COLS], F32)
-            nc.scalar.activation(out=outer[:], in_=neg_m[:], func=ACT.Square, scale=math.sqrt(4.0 / 3.0))
+            nc.scalar.activation(out=outer[:], in_=half_s[:], func=ACT.Square, scale=1.0, bias=-1.0)
             inner = work.tile([P, FOLDS, TILE_COLS], F32)
-            nc.scalar.activation(out=inner[:], in_=neg_m[:], func=ACT.Square, scale=2.0, bias=2.0)
-            nc.vector.scalar_tensor_tensor(
-                out=outer[:], in0=outer[:], scalar=-1.0, in1=neg_m[:], op0=ALU.mult, op1=ALU.mult
-            )
-            nc.vector.tensor_tensor(out=inner[:], in0=inner[:], in1=neg_m[:], op=ALU.mult)
-            value = work.tile([P, FOLDS, TILE_COLS], BF16)
-            nc.vector.scalar_tensor_tensor(
-                out=value[:], in0=inner[:], scalar=2.0 / 3.0, in1=outer[:], op0=ALU.add, op1=ALU.min
-            )
-            below = work.tile([P, FOLDS, TILE_COLS], BF16)
-            for r in range(FOLDS):
-                nc.vector.tensor_scalar(
-                    out=below[:, r, :], in0=x_tile, scalar1=(r - 1.5) / 2.5, scalar2=None, op0=ALU.is_lt
-                )
-            low = work.tile([P, FOLDS, TILE_COLS], BF16, align_bytes=64)
-            nc.vector.tensor_tensor(out=low[:], in0=value[:], in1=below[:], op=ALU.mult)
-            high = work.tile([P, FOLDS, TILE_COLS], BF16, align_bytes=64)
-            nc.vector.tensor_tensor(out=high[:], in0=value[:], in1=low[:], op=ALU.subtract)
+            nc.scalar.activation(out=inner[:], in_=half_s[:], func=ACT.Square, scale=2.0)
+            return half_s, outer, inner
 
-            b_codes = codes.tile([P, SPLINES, P], U32, align_bytes=64)
-            b_scales = codes.tile([P, SPLINES, P], U8, align_bytes=64)
-            for half, splines in ((0, low), (1, high)):
-                l0 = half * FOLDS
-                nc.vector.quantize_mx(
-                    out=b_codes[:, l0 : l0 + FOLDS, :].rearrange("p l b -> p (l b)").bitcast(FP8X4),
-                    scales=b_scales[:, l0 : l0 + FOLDS, :].rearrange("p l b -> p (l b)"),
-                    in_=splines[:].rearrange("p r c -> p (r c)"),
-                )
+        def quantise_splines(four_splines, b_codes, b_scales, l0):
+            nc.vector.quantize_mx(
+                out=b_codes[:, l0 : l0 + FOLDS, :].rearrange("p l b -> p (l b)").bitcast(FP8X4),
+                scales=b_scales[:, l0 : l0 + FOLDS, :].rearrange("p l b -> p (l b)"),
+                in_=four_splines[:].rearrange("p r c -> p (r c)"),
+            )
 
+        def multiply(j, b_codes, b_scales):
             acc = sums.tile([P, OUTS], F32)
             nc.tensor.matmul_mx(
                 out=acc[:],
@@ -169,3 +165,50 @@ def tile_kanlayer_kernel(tc, x, base_weight_words, base_weight_scales, spline_we
             result = results.tile([P, OUTS], F32)
             nc.scalar.copy(out=result[:], in_=acc[:])
             nc.sync.dma_start(out=out_rows[:, j, :], in_=result[:])
+
+        basis_codes = {}
+        ahead = scalar_stage(0)
+        for j in range(ROW_TILES):
+            half_s, outer, inner = ahead
+            if j < OUT_TILES:
+                pairs = turn_weights(j)
+            if j + 1 < ROW_TILES:
+                ahead = scalar_stage(j + 1)
+
+            neg_m = work.tile([P, FOLDS, TILE_COLS], F32)
+            nc.vector.tensor_scalar(out=neg_m[:], in0=half_s[:], scalar1=1.0, scalar2=-1.0, op0=ALU.min, op1=ALU.add)
+            x_tile = x_safe[:, j, :, :].rearrange("p b t -> p (b t)")
+            below = work.tile([P, FOLDS, TILE_COLS], BF16)
+            for r in range(FOLDS):
+                nc.vector.tensor_scalar(
+                    out=below[:, r, :], in0=x_tile, scalar1=(r - 1.5) / 2.5, scalar2=None, op0=ALU.is_lt
+                )
+            nc.vector.scalar_tensor_tensor(
+                out=outer[:], in0=outer[:], scalar=-4.0 / 3.0, in1=neg_m[:], op0=ALU.mult, op1=ALU.mult
+            )
+            nc.vector.tensor_tensor(out=inner[:], in0=inner[:], in1=neg_m[:], op=ALU.mult)
+            if j > 0:
+                quantise_splines(low, b_codes, b_scales, 0)
+            value = work.tile([P, FOLDS, TILE_COLS], BF16)
+            nc.vector.scalar_tensor_tensor(
+                out=value[:], in0=inner[:], scalar=2.0 / 3.0, in1=outer[:], op0=ALU.add, op1=ALU.min
+            )
+            if j > 0:
+                quantise_splines(high, b_codes, b_scales, FOLDS)
+            low = work.tile([P, FOLDS, TILE_COLS], BF16, align_bytes=64)
+            nc.vector.tensor_tensor(out=low[:], in0=value[:], in1=below[:], op=ALU.mult)
+            if j < OUT_TILES:
+                quantise_weights(j, pairs)
+            high = work.tile([P, FOLDS, TILE_COLS], BF16, align_bytes=64)
+            nc.vector.tensor_tensor(out=high[:], in0=value[:], in1=low[:], op=ALU.subtract)
+            b_codes = codes.tile([P, SPLINES, P], U32, align_bytes=64)
+            b_scales = codes.tile([P, SPLINES, P], U8, align_bytes=64)
+            basis_codes[j] = (b_codes, b_scales)
+
+            if j >= MULTIPLY_LAG:
+                multiply(j - MULTIPLY_LAG, basis_codes[j - MULTIPLY_LAG][0], basis_codes[j - MULTIPLY_LAG][1])
+
+        quantise_splines(low, b_codes, b_scales, 0)
+        quantise_splines(high, b_codes, b_scales, FOLDS)
+        for j in range(ROW_TILES - MULTIPLY_LAG, ROW_TILES):
+            multiply(j, basis_codes[j][0], basis_codes[j][1])

@@ -24,8 +24,12 @@ ROW_TILES = BATCH // P
 OUT_TILES = OUTS // P
 TILE_COLS = P * PACK
 WORDS_PER_FEATURE = SPLINES // 2
-MULTIPLY_LAG = OUT_TILES - 1
+WEIGHT_UNITS = OUT_TILES * WORDS_PER_FEATURE
+UNITS_PER_ROW_TILE = 3
+MULTIPLY_LAG = (WEIGHT_UNITS - 1) // UNITS_PER_ROW_TILE
 X_BOUND = 4.0
+ROOT = (2.0 ** (1.0 / 3.0) + 2.0 ** (-1.0 / 3.0) - 1.0) / 3.0
+REST = 4.0 * (ROOT * ROOT + ROOT) - (1.0 + ROOT) ** 2
 
 FLOPS = 2 * BATCH * OUTS * (FEATURES + FEATURES * SPLINES)
 
@@ -34,11 +38,12 @@ def tile_kanlayer_kernel(tc, x, base_weight_words, base_weight_scales, spline_we
     nc = tc.nc
     with ExitStack() as ctx:
         keep = ctx.enter_context(tc.tile_pool(name="keep", bufs=1))
-        weight_stage = ctx.enter_context(tc.tile_pool(name="weight_stage", bufs=WORDS_PER_FEATURE))
+        weight_stage = ctx.enter_context(tc.tile_pool(name="weight_stage", bufs=2 * UNITS_PER_ROW_TILE))
         work = ctx.enter_context(tc.tile_pool(name="work", bufs=2))
+        scratch = ctx.enter_context(tc.tile_pool(name="scratch", bufs=1))
         codes = ctx.enter_context(tc.tile_pool(name="codes", bufs=MULTIPLY_LAG + 2))
         results = ctx.enter_context(tc.tile_pool(name="results", bufs=3))
-        turned = ctx.enter_context(tc.psum_pool(name="turned", bufs=WORDS_PER_FEATURE))
+        turned = ctx.enter_context(tc.psum_pool(name="turned", bufs=4))
         sums = ctx.enter_context(tc.psum_pool(name="sums", bufs=3))
         ctx.enter_context(tc.manual_schedule())
 
@@ -99,28 +104,26 @@ def tile_kanlayer_kernel(tc, x, base_weight_words, base_weight_scales, spline_we
         w_codes = keep.tile([P, SPLINES, OUTS], U32, align_bytes=64)
         w_scales = keep.tile([P, SPLINES, OUTS], U8, align_bytes=64)
 
-        def turn_weights(c):
-            pairs = []
-            for w in range(WORDS_PER_FEATURE):
-                wt = turned.tile([P, PACK, P], F32, tag="turned")
-                for t in range(PACK):
-                    first_word = WORDS_PER_FEATURE * t + w
-                    nc.tensor.transpose(
-                        wt[:, t, :], w_words[:, c, first_word : words_in_row : WORDS_PER_FEATURE * PACK], ident[:]
-                    )
-                w_grouped = weight_stage.tile([P, 2, P, PACK], BF16, align_bytes=64)
-                nc.scalar.copy(out=w_grouped[:], in_=wt[:].bitcast(BF16).rearrange("p t (o e) -> p e o t", e=2))
-                pairs.append(w_grouped)
-            return pairs
+        def turn_unit(unit):
+            c, w = divmod(unit, WORDS_PER_FEATURE)
+            wt = turned.tile([P, PACK, P], F32, tag="turned")
+            for t in range(PACK):
+                first_word = WORDS_PER_FEATURE * t + w
+                nc.tensor.transpose(
+                    wt[:, t, :], w_words[:, c, first_word : words_in_row : WORDS_PER_FEATURE * PACK], ident[:]
+                )
+            w_grouped = weight_stage.tile([P, 2, P, PACK], BF16, align_bytes=64)
+            nc.scalar.copy(out=w_grouped[:], in_=wt[:].bitcast(BF16).rearrange("p t (o e) -> p e o t", e=2))
+            return w_grouped
 
-        def quantise_weights(c, pairs):
-            for w in range(WORDS_PER_FEATURE):
-                for e in range(2):
-                    nc.vector.quantize_mx(
-                        out=w_codes[:, 2 * w + e, c * P : (c + 1) * P].bitcast(FP8X4),
-                        scales=w_scales[:, 2 * w + e, c * P : (c + 1) * P],
-                        in_=pairs[w][:, e, :, :].rearrange("p o t -> p (o t)"),
-                    )
+        def quantise_unit(unit, w_grouped):
+            c, w = divmod(unit, WORDS_PER_FEATURE)
+            for e in range(2):
+                nc.vector.quantize_mx(
+                    out=w_codes[:, 2 * w + e, c * P : (c + 1) * P].bitcast(FP8X4),
+                    scales=w_scales[:, 2 * w + e, c * P : (c + 1) * P],
+                    in_=w_grouped[:, e, :, :].rearrange("p o t -> p (o t)"),
+                )
 
         def scalar_stage(j):
             x_tile = x_safe[:, j, :, :].rearrange("p b t -> p (b t)")
@@ -129,9 +132,11 @@ def tile_kanlayer_kernel(tc, x, base_weight_words, base_weight_scales, spline_we
                 nc.scalar.activation(out=half_s[:, r, :], in_=x_tile, func=ACT.Abs, scale=1.25, bias=(1.5 - r) / 2.0)
             nc.scalar.activation(out=half_s[:], in_=half_s[:], func=ACT.Abs, scale=1.0, bias=-1.0)
             outer = work.tile([P, FOLDS, TILE_COLS], F32)
-            nc.scalar.activation(out=outer[:], in_=half_s[:], func=ACT.Square, scale=1.0, bias=-1.0)
+            nc.scalar.activation(
+                out=outer[:], in_=half_s[:], func=ACT.Square, scale=math.sqrt(4.0 / 3.0), bias=-math.sqrt(4.0 / 3.0)
+            )
             inner = work.tile([P, FOLDS, TILE_COLS], F32)
-            nc.scalar.activation(out=inner[:], in_=half_s[:], func=ACT.Square, scale=2.0)
+            nc.scalar.activation(out=inner[:], in_=half_s[:], func=ACT.Square, scale=2.0, bias=-(1.0 + ROOT))
             return half_s, outer, inner
 
         def quantise_splines(four_splines, b_codes, b_scales, l0):
@@ -170,35 +175,40 @@ def tile_kanlayer_kernel(tc, x, base_weight_words, base_weight_scales, spline_we
         ahead = scalar_stage(0)
         for j in range(ROW_TILES):
             half_s, outer, inner = ahead
-            if j < OUT_TILES:
-                pairs = turn_weights(j)
+            units = range(j * UNITS_PER_ROW_TILE, min((j + 1) * UNITS_PER_ROW_TILE, WEIGHT_UNITS))
+            grouped = [turn_unit(unit) for unit in units]
             if j + 1 < ROW_TILES:
                 ahead = scalar_stage(j + 1)
 
-            neg_m = work.tile([P, FOLDS, TILE_COLS], F32)
-            nc.vector.tensor_scalar(out=neg_m[:], in0=half_s[:], scalar1=1.0, scalar2=-1.0, op0=ALU.min, op1=ALU.add)
+            shifted = scratch.tile([P, FOLDS, TILE_COLS], F32)
+            nc.vector.tensor_scalar(
+                out=shifted[:], in0=half_s[:], scalar1=ROOT, scalar2=1.0 + ROOT, op0=ALU.add, op1=ALU.min
+            )
             x_tile = x_safe[:, j, :, :].rearrange("p b t -> p (b t)")
-            below = work.tile([P, FOLDS, TILE_COLS], BF16)
+            below = scratch.tile([P, FOLDS, TILE_COLS], BF16)
             for r in range(FOLDS):
                 nc.vector.tensor_scalar(
                     out=below[:, r, :], in0=x_tile, scalar1=(r - 1.5) / 2.5, scalar2=None, op0=ALU.is_lt
                 )
+            outer_piece = scratch.tile([P, FOLDS, TILE_COLS], BF16)
             nc.vector.scalar_tensor_tensor(
-                out=outer[:], in0=outer[:], scalar=-4.0 / 3.0, in1=neg_m[:], op0=ALU.mult, op1=ALU.mult
+                out=outer_piece[:], in0=shifted[:], scalar=1.0 + ROOT, in1=outer[:], op0=ALU.subtract, op1=ALU.mult
             )
-            nc.vector.tensor_tensor(out=inner[:], in0=inner[:], in1=neg_m[:], op=ALU.mult)
+            inner_piece = scratch.tile([P, FOLDS, TILE_COLS], BF16)
+            nc.vector.scalar_tensor_tensor(
+                out=inner_piece[:], in0=inner[:], scalar=REST, in1=shifted[:], op0=ALU.add, op1=ALU.mult
+            )
+            nc.vector.tensor_scalar(out=outer_piece[:], in0=outer_piece[:], scalar1=-1.0, scalar2=None, op0=ALU.mult)
             if j > 0:
                 quantise_splines(low, b_codes, b_scales, 0)
-            value = work.tile([P, FOLDS, TILE_COLS], BF16)
-            nc.vector.scalar_tensor_tensor(
-                out=value[:], in0=inner[:], scalar=2.0 / 3.0, in1=outer[:], op0=ALU.add, op1=ALU.min
-            )
+            value = scratch.tile([P, FOLDS, TILE_COLS], BF16)
+            nc.vector.tensor_tensor(out=value[:], in0=outer_piece[:], in1=inner_piece[:], op=ALU.min)
             if j > 0:
                 quantise_splines(high, b_codes, b_scales, FOLDS)
             low = work.tile([P, FOLDS, TILE_COLS], BF16, align_bytes=64)
             nc.vector.tensor_tensor(out=low[:], in0=value[:], in1=below[:], op=ALU.mult)
-            if j < OUT_TILES:
-                quantise_weights(j, pairs)
+            for unit, w_grouped in zip(units, grouped):
+                quantise_unit(unit, w_grouped)
             high = work.tile([P, FOLDS, TILE_COLS], BF16, align_bytes=64)
             nc.vector.tensor_tensor(out=high[:], in0=value[:], in1=low[:], op=ALU.subtract)
             b_codes = codes.tile([P, SPLINES, P], U32, align_bytes=64)

@@ -27,9 +27,6 @@ WORDS_PER_FEATURE = SPLINES // 2
 WEIGHT_UNITS = OUT_TILES * WORDS_PER_FEATURE
 UNITS_PER_ROW_TILE = 3
 MULTIPLY_LAG = (WEIGHT_UNITS - 1) // UNITS_PER_ROW_TILE
-X_BOUND = 4.0
-ROOT = (2.0 ** (1.0 / 3.0) + 2.0 ** (-1.0 / 3.0) - 1.0) / 3.0
-REST = 4.0 * (ROOT * ROOT + ROOT) - (1.0 + ROOT) ** 2
 
 FLOPS = 2 * BATCH * OUTS * (FEATURES + FEATURES * SPLINES)
 
@@ -75,21 +72,12 @@ def tile_kanlayer_kernel(tc, x, base_weight_words, base_weight_scales, spline_we
         x_words = x_sb[:].bitcast(F32)
         x_turned = keep.tile([P, ROW_TILES, P, PACK], BF16, align_bytes=64)
         x_turned_words = x_turned[:].bitcast(F32)
-        x_safe = keep.tile([P, ROW_TILES, P, PACK], BF16)
         for j in range(0, ROW_TILES, 2):
             xt = turned.tile([P, 2, 2, P], F32, tag="turned")
             for k in range(2):
                 for u in range(2):
                     nc.tensor.transpose(xt[:, k, u, :], x_words[:, j + k, u : FEATURES // 2 : 2], ident[:])
             nc.vector.tensor_copy(out=x_turned_words[:, j : j + 2, :, :], in_=xt[:].rearrange("p k u b -> p k b u"))
-            nc.vector.tensor_scalar(
-                out=x_safe[:, j : j + 2, :, :],
-                in0=x_turned[:, j : j + 2, :, :],
-                scalar1=-X_BOUND,
-                scalar2=X_BOUND,
-                op0=ALU.max,
-                op1=ALU.min,
-            )
 
         x_codes = keep.tile([P, ROW_TILES * P], U32, align_bytes=64)
         x_scales = keep.tile([P, ROW_TILES * P], U8, align_bytes=64)
@@ -126,18 +114,25 @@ def tile_kanlayer_kernel(tc, x, base_weight_words, base_weight_scales, spline_we
                 )
 
         def scalar_stage(j):
-            x_tile = x_safe[:, j, :, :].rearrange("p b t -> p (b t)")
+            x_tile = x_turned[:, j, :, :].rearrange("p b t -> p (b t)")
             half_s = work.tile([P, FOLDS, TILE_COLS], F32)
             for r in range(FOLDS):
                 nc.scalar.activation(out=half_s[:, r, :], in_=x_tile, func=ACT.Abs, scale=1.25, bias=(1.5 - r) / 2.0)
             nc.scalar.activation(out=half_s[:], in_=half_s[:], func=ACT.Abs, scale=1.0, bias=-1.0)
-            outer = work.tile([P, FOLDS, TILE_COLS], F32)
+            four_m2 = work.tile([P, FOLDS, TILE_COLS], F32)
+            nc.scalar.activation(out=four_m2[:], in_=half_s[:], func=ACT.Square, scale=2.0, bias=-2.0)
+            bowl = work.tile([P, FOLDS, TILE_COLS], F32)
             nc.scalar.activation(
-                out=outer[:], in_=half_s[:], func=ACT.Square, scale=math.sqrt(4.0 / 3.0), bias=-math.sqrt(4.0 / 3.0)
+                out=bowl[:], in_=half_s[:], func=ACT.Square, scale=math.sqrt(8.0), bias=-0.75 * math.sqrt(8.0)
             )
-            inner = work.tile([P, FOLDS, TILE_COLS], F32)
-            nc.scalar.activation(out=inner[:], in_=half_s[:], func=ACT.Square, scale=2.0, bias=-(1.0 + ROOT))
-            return half_s, outer, inner
+            return half_s, four_m2, bowl
+
+        def make_cube(half_s, four_m2):
+            cube = scratch.tile([P, FOLDS, TILE_COLS], F32)
+            nc.vector.scalar_tensor_tensor(
+                out=cube[:], in0=half_s[:], scalar=1.0, in1=four_m2[:], op0=ALU.subtract, op1=ALU.mult
+            )
+            return cube
 
         def quantise_splines(four_splines, b_codes, b_scales, l0):
             nc.vector.quantize_mx(
@@ -173,42 +168,40 @@ def tile_kanlayer_kernel(tc, x, base_weight_words, base_weight_scales, spline_we
 
         basis_codes = {}
         ahead = scalar_stage(0)
+        cube = make_cube(ahead[0], ahead[1])
         for j in range(ROW_TILES):
-            half_s, outer, inner = ahead
+            bowl = ahead[2]
             units = range(j * UNITS_PER_ROW_TILE, min((j + 1) * UNITS_PER_ROW_TILE, WEIGHT_UNITS))
             grouped = [turn_unit(unit) for unit in units]
             if j + 1 < ROW_TILES:
                 ahead = scalar_stage(j + 1)
 
-            shifted = scratch.tile([P, FOLDS, TILE_COLS], F32)
-            nc.vector.tensor_scalar(
-                out=shifted[:], in0=half_s[:], scalar1=ROOT, scalar2=1.0 + ROOT, op0=ALU.add, op1=ALU.min
-            )
-            x_tile = x_safe[:, j, :, :].rearrange("p b t -> p (b t)")
+            x_tile = x_turned[:, j, :, :].rearrange("p b t -> p (b t)")
             below = scratch.tile([P, FOLDS, TILE_COLS], BF16)
             for r in range(FOLDS):
                 nc.vector.tensor_scalar(
                     out=below[:, r, :], in0=x_tile, scalar1=(r - 1.5) / 2.5, scalar2=None, op0=ALU.is_lt
                 )
-            outer_piece = scratch.tile([P, FOLDS, TILE_COLS], BF16)
+            inner = scratch.tile([P, FOLDS, TILE_COLS], BF16)
             nc.vector.scalar_tensor_tensor(
-                out=outer_piece[:], in0=shifted[:], scalar=1.0 + ROOT, in1=outer[:], op0=ALU.subtract, op1=ALU.mult
+                out=inner[:], in0=bowl[:], scalar=1.0 / 6.0, in1=cube[:], op0=ALU.add, op1=ALU.add
             )
-            inner_piece = scratch.tile([P, FOLDS, TILE_COLS], BF16)
-            nc.vector.scalar_tensor_tensor(
-                out=inner_piece[:], in0=inner[:], scalar=REST, in1=shifted[:], op0=ALU.add, op1=ALU.mult
+            outer = scratch.tile([P, FOLDS, TILE_COLS], BF16)
+            nc.vector.tensor_scalar(
+                out=outer[:], in0=cube[:], scalar1=-1.0 / 3.0, scalar2=0.0, op0=ALU.mult, op1=ALU.max
             )
-            nc.vector.tensor_scalar(out=outer_piece[:], in0=outer_piece[:], scalar1=-1.0, scalar2=None, op0=ALU.mult)
             if j > 0:
                 quantise_splines(low, b_codes, b_scales, 0)
             value = scratch.tile([P, FOLDS, TILE_COLS], BF16)
-            nc.vector.tensor_tensor(out=value[:], in0=outer_piece[:], in1=inner_piece[:], op=ALU.min)
+            nc.vector.tensor_tensor(out=value[:], in0=outer[:], in1=inner[:], op=ALU.min)
             if j > 0:
                 quantise_splines(high, b_codes, b_scales, FOLDS)
-            low = work.tile([P, FOLDS, TILE_COLS], BF16, align_bytes=64)
-            nc.vector.tensor_tensor(out=low[:], in0=value[:], in1=below[:], op=ALU.mult)
             for unit, w_grouped in zip(units, grouped):
                 quantise_unit(unit, w_grouped)
+            low = work.tile([P, FOLDS, TILE_COLS], BF16, align_bytes=64)
+            nc.vector.tensor_tensor(out=low[:], in0=value[:], in1=below[:], op=ALU.mult)
+            if j + 1 < ROW_TILES:
+                cube = make_cube(ahead[0], ahead[1])
             high = work.tile([P, FOLDS, TILE_COLS], BF16, align_bytes=64)
             nc.vector.tensor_tensor(out=high[:], in0=value[:], in1=low[:], op=ALU.subtract)
             b_codes = codes.tile([P, SPLINES, P], U32, align_bytes=64)

@@ -26,7 +26,10 @@ TILE_COLS = P * PACK
 WORDS_PER_FEATURE = SPLINES // 2
 WEIGHT_UNITS = OUT_TILES * WORDS_PER_FEATURE
 UNITS_PER_ROW_TILE = 3
+VECTOR_UNIT_STRIDE = 4
 MULTIPLY_LAG = (WEIGHT_UNITS - 1) // UNITS_PER_ROW_TILE
+ROOT = (2.0 ** (1.0 / 3.0) + 2.0 ** (-1.0 / 3.0) - 1.0) / 3.0
+REST = 4.0 * (ROOT * ROOT + ROOT) - (1.0 + ROOT) ** 2
 
 FLOPS = 2 * BATCH * OUTS * (FEATURES + FEATURES * SPLINES)
 
@@ -101,7 +104,11 @@ def tile_kanlayer_kernel(tc, x, base_weight_words, base_weight_scales, spline_we
                     wt[:, t, :], w_words[:, c, first_word : words_in_row : WORDS_PER_FEATURE * PACK], ident[:]
                 )
             w_grouped = weight_stage.tile([P, 2, P, PACK], BF16, align_bytes=64)
-            nc.scalar.copy(out=w_grouped[:], in_=wt[:].bitcast(BF16).rearrange("p t (o e) -> p e o t", e=2))
+            pairs = wt[:].bitcast(BF16).rearrange("p t (o e) -> p e o t", e=2)
+            if unit % VECTOR_UNIT_STRIDE == VECTOR_UNIT_STRIDE - 1:
+                nc.vector.tensor_copy(out=w_grouped[:], in_=pairs)
+            else:
+                nc.scalar.copy(out=w_grouped[:], in_=pairs)
             return w_grouped
 
         def quantise_unit(unit, w_grouped):
@@ -119,20 +126,22 @@ def tile_kanlayer_kernel(tc, x, base_weight_words, base_weight_scales, spline_we
             for r in range(FOLDS):
                 nc.scalar.activation(out=half_s[:, r, :], in_=x_tile, func=ACT.Abs, scale=1.25, bias=(1.5 - r) / 2.0)
             nc.scalar.activation(out=half_s[:], in_=half_s[:], func=ACT.Abs, scale=1.0, bias=-1.0)
-            four_m2 = work.tile([P, FOLDS, TILE_COLS], F32)
-            nc.scalar.activation(out=four_m2[:], in_=half_s[:], func=ACT.Square, scale=2.0, bias=-2.0)
-            bowl = work.tile([P, FOLDS, TILE_COLS], F32)
+            nearest = work.tile([P, 2, TILE_COLS], F32)
+            nc.scalar.activation(out=nearest[:], in_=half_s[:, 1:3, :], func=ACT.Abs, scale=2.0, bias=-1.0)
+            outer_sq = work.tile([P, FOLDS, TILE_COLS], F32)
             nc.scalar.activation(
-                out=bowl[:], in_=half_s[:], func=ACT.Square, scale=math.sqrt(8.0), bias=-0.75 * math.sqrt(8.0)
+                out=outer_sq[:], in_=half_s[:], func=ACT.Square, scale=math.sqrt(4.0 / 3.0), bias=-math.sqrt(4.0 / 3.0)
             )
-            return half_s, four_m2, bowl
+            inner_sq = work.tile([P, 2, TILE_COLS], F32)
+            nc.scalar.activation(out=inner_sq[:], in_=nearest[:], func=ACT.Square, scale=1.0, bias=-(1.0 + ROOT))
+            return half_s, outer_sq, nearest, inner_sq
 
-        def make_cube(half_s, four_m2):
-            cube = scratch.tile([P, FOLDS, TILE_COLS], F32)
+        def make_minus_outer(half_s, outer_sq):
+            minus_outer = scratch.tile([P, FOLDS, TILE_COLS], BF16)
             nc.vector.scalar_tensor_tensor(
-                out=cube[:], in0=half_s[:], scalar=1.0, in1=four_m2[:], op0=ALU.subtract, op1=ALU.mult
+                out=minus_outer[:], in0=half_s[:], scalar=1.0, in1=outer_sq[:], op0=ALU.subtract, op1=ALU.mult
             )
-            return cube
+            return minus_outer
 
         def quantise_splines(four_splines, b_codes, b_scales, l0):
             nc.vector.quantize_mx(
@@ -168,32 +177,41 @@ def tile_kanlayer_kernel(tc, x, base_weight_words, base_weight_scales, spline_we
 
         basis_codes = {}
         ahead = scalar_stage(0)
-        cube = make_cube(ahead[0], ahead[1])
+        minus_outer = make_minus_outer(ahead[0], ahead[1])
         for j in range(ROW_TILES):
-            bowl = ahead[2]
+            nearest, inner_sq = ahead[2], ahead[3]
             units = range(j * UNITS_PER_ROW_TILE, min((j + 1) * UNITS_PER_ROW_TILE, WEIGHT_UNITS))
             grouped = [turn_unit(unit) for unit in units]
             if j + 1 < ROW_TILES:
                 ahead = scalar_stage(j + 1)
 
+            shifted = scratch.tile([P, 2, TILE_COLS], F32)
+            nc.vector.tensor_scalar(
+                out=shifted[:], in0=nearest[:], scalar1=0.5, scalar2=ROOT, op0=ALU.mult, op1=ALU.add
+            )
             x_tile = x_turned[:, j, :, :].rearrange("p b t -> p (b t)")
             below = scratch.tile([P, FOLDS, TILE_COLS], BF16)
             for r in range(FOLDS):
                 nc.vector.tensor_scalar(
                     out=below[:, r, :], in0=x_tile, scalar1=(r - 1.5) / 2.5, scalar2=None, op0=ALU.is_lt
                 )
-            inner = scratch.tile([P, FOLDS, TILE_COLS], BF16)
+            inner = scratch.tile([P, 2, TILE_COLS], BF16)
             nc.vector.scalar_tensor_tensor(
-                out=inner[:], in0=bowl[:], scalar=1.0 / 6.0, in1=cube[:], op0=ALU.add, op1=ALU.add
+                out=inner[:], in0=inner_sq[:], scalar=REST, in1=shifted[:], op0=ALU.add, op1=ALU.mult
             )
             outer = scratch.tile([P, FOLDS, TILE_COLS], BF16)
             nc.vector.tensor_scalar(
-                out=outer[:], in0=cube[:], scalar1=-1.0 / 3.0, scalar2=0.0, op0=ALU.mult, op1=ALU.max
+                out=outer[:], in0=minus_outer[:], scalar1=-1.0, scalar2=0.0, op0=ALU.mult, op1=ALU.max
             )
             if j > 0:
                 quantise_splines(low, b_codes, b_scales, 0)
             value = scratch.tile([P, FOLDS, TILE_COLS], BF16)
-            nc.vector.tensor_tensor(out=value[:], in0=outer[:], in1=inner[:], op=ALU.min)
+            nc.vector.tensor_tensor(
+                out=value[:].rearrange("p (h g) c -> p h (g c)", g=2),
+                in0=outer[:].rearrange("p (h g) c -> p h (g c)", g=2),
+                in1=inner[:].rearrange("p g c -> p (g c)").unsqueeze(1).to_broadcast([P, 2, 2 * TILE_COLS]),
+                op=ALU.min,
+            )
             if j > 0:
                 quantise_splines(high, b_codes, b_scales, FOLDS)
             for unit, w_grouped in zip(units, grouped):
@@ -201,7 +219,7 @@ def tile_kanlayer_kernel(tc, x, base_weight_words, base_weight_scales, spline_we
             low = work.tile([P, FOLDS, TILE_COLS], BF16, align_bytes=64)
             nc.vector.tensor_tensor(out=low[:], in0=value[:], in1=below[:], op=ALU.mult)
             if j + 1 < ROW_TILES:
-                cube = make_cube(ahead[0], ahead[1])
+                minus_outer = make_minus_outer(ahead[0], ahead[1])
             high = work.tile([P, FOLDS, TILE_COLS], BF16, align_bytes=64)
             nc.vector.tensor_tensor(out=high[:], in0=value[:], in1=low[:], op=ALU.subtract)
             b_codes = codes.tile([P, SPLINES, P], U32, align_bytes=64)

@@ -26,7 +26,7 @@ TILE_COLS = P * PACK
 WORDS_PER_FEATURE = SPLINES // 2
 WEIGHT_UNITS = OUT_TILES * WORDS_PER_FEATURE
 UNITS_PER_ROW_TILE = 3
-VECTOR_UNIT_STRIDE = 4
+VECTOR_UNITS = 4
 MULTIPLY_LAG = (WEIGHT_UNITS - 1) // UNITS_PER_ROW_TILE
 ROOT = (2.0 ** (1.0 / 3.0) + 2.0 ** (-1.0 / 3.0) - 1.0) / 3.0
 REST = 4.0 * (ROOT * ROOT + ROOT) - (1.0 + ROOT) ** 2
@@ -105,7 +105,7 @@ def tile_kanlayer_kernel(tc, x, base_weight_words, base_weight_scales, spline_we
                 )
             w_grouped = weight_stage.tile([P, 2, P, PACK], BF16, align_bytes=64)
             pairs = wt[:].bitcast(BF16).rearrange("p t (o e) -> p e o t", e=2)
-            if unit % VECTOR_UNIT_STRIDE == VECTOR_UNIT_STRIDE - 1:
+            if unit < VECTOR_UNITS:
                 nc.vector.tensor_copy(out=w_grouped[:], in_=pairs)
             else:
                 nc.scalar.copy(out=w_grouped[:], in_=pairs)
@@ -120,28 +120,34 @@ def tile_kanlayer_kernel(tc, x, base_weight_words, base_weight_scales, spline_we
                     in_=w_grouped[:, e, :, :].rearrange("p o t -> p (o t)"),
                 )
 
-        def scalar_stage(j):
-            x_tile = x_turned[:, j, :, :].rearrange("p b t -> p (b t)")
+        def scalar_tiles():
             half_s = work.tile([P, FOLDS, TILE_COLS], F32)
-            for r in range(FOLDS):
-                nc.scalar.activation(out=half_s[:, r, :], in_=x_tile, func=ACT.Abs, scale=1.25, bias=(1.5 - r) / 2.0)
-            nc.scalar.activation(out=half_s[:], in_=half_s[:], func=ACT.Abs, scale=1.0, bias=-1.0)
-            nearest = work.tile([P, 2, TILE_COLS], F32)
-            nc.scalar.activation(out=nearest[:], in_=half_s[:, 1:3, :], func=ACT.Abs, scale=2.0, bias=-1.0)
             outer_sq = work.tile([P, FOLDS, TILE_COLS], F32)
-            nc.scalar.activation(
-                out=outer_sq[:], in_=half_s[:], func=ACT.Square, scale=math.sqrt(4.0 / 3.0), bias=-math.sqrt(4.0 / 3.0)
-            )
+            nearest = work.tile([P, 2, TILE_COLS], F32)
             inner_sq = work.tile([P, 2, TILE_COLS], F32)
-            nc.scalar.activation(out=inner_sq[:], in_=nearest[:], func=ACT.Square, scale=1.0, bias=-(1.0 + ROOT))
             return half_s, outer_sq, nearest, inner_sq
 
-        def make_minus_outer(half_s, outer_sq):
-            minus_outer = scratch.tile([P, FOLDS, TILE_COLS], BF16)
-            nc.vector.scalar_tensor_tensor(
-                out=minus_outer[:], in0=half_s[:], scalar=1.0, in1=outer_sq[:], op0=ALU.subtract, op1=ALU.mult
+        def scalar_stage(j, cols, tiles):
+            half_s, outer_sq, nearest, inner_sq = tiles
+            x_tile = x_turned[:, j, :, :].rearrange("p b t -> p (b t)")[:, cols]
+            for r in range(FOLDS):
+                nc.scalar.activation(
+                    out=half_s[:, r, cols], in_=x_tile, func=ACT.Abs, scale=1.25, bias=(1.5 - r) / 2.0
+                )
+            nc.scalar.activation(out=half_s[:, :, cols], in_=half_s[:, :, cols], func=ACT.Abs, scale=1.0, bias=-1.0)
+            nc.scalar.activation(
+                out=outer_sq[:, :, cols],
+                in_=half_s[:, :, cols],
+                func=ACT.Square,
+                scale=math.sqrt(4.0 / 3.0),
+                bias=-math.sqrt(4.0 / 3.0),
             )
-            return minus_outer
+            nc.scalar.activation(
+                out=nearest[:, :, cols], in_=half_s[:, 1:3, cols], func=ACT.Abs, scale=2.0, bias=-1.0
+            )
+            nc.scalar.activation(
+                out=inner_sq[:, :, cols], in_=nearest[:, :, cols], func=ACT.Square, scale=1.0, bias=-(1.0 + ROOT)
+            )
 
         def quantise_splines(four_splines, b_codes, b_scales, l0):
             nc.vector.quantize_mx(
@@ -150,86 +156,155 @@ def tile_kanlayer_kernel(tc, x, base_weight_words, base_weight_scales, spline_we
                 in_=four_splines[:].rearrange("p r c -> p (r c)"),
             )
 
-        def multiply(j, b_codes, b_scales):
-            acc = sums.tile([P, OUTS], F32)
+        basis_codes = {}
+
+        def x_pass(acc, outs, j):
             nc.tensor.matmul_mx(
-                out=acc[:],
+                out=acc[:, outs],
                 lhsT=x_codes[:, j * P : (j + 1) * P].bitcast(FP8X4),
                 lhsT_scale=x_scales[:, j * P : (j + 1) * P],
-                rhs=base_codes[:].bitcast(FP8X4),
-                rhs_scale=base_scales[:],
+                rhs=base_codes[:, outs].bitcast(FP8X4),
+                rhs_scale=base_scales[:, outs],
                 start=True,
                 stop=False,
             )
-            for l in range(SPLINES):
+
+        def spline_passes(acc, outs, j, splines):
+            b_codes, b_scales = basis_codes[j]
+            for l in splines:
                 nc.tensor.matmul_mx(
-                    out=acc[:],
+                    out=acc[:, outs],
                     lhsT=b_codes[:, l, :].bitcast(FP8X4),
                     lhsT_scale=b_scales[:, l, :],
-                    rhs=w_codes[:, l, :].bitcast(FP8X4),
-                    rhs_scale=w_scales[:, l, :],
+                    rhs=w_codes[:, l, outs].bitcast(FP8X4),
+                    rhs_scale=w_scales[:, l, outs],
                     start=False,
                     stop=(l == SPLINES - 1),
                 )
-            result = results.tile([P, OUTS], F32)
+
+        def multiply(j):
+            acc = sums.tile([P, OUTS], F32, name="acc")
+            x_pass(acc, slice(0, OUTS), j)
+            spline_passes(acc, slice(0, OUTS), j, range(SPLINES))
+            result = results.tile([P, OUTS], F32, name="result")
             nc.scalar.copy(out=result[:], in_=acc[:])
             nc.sync.dma_start(out=out_rows[:, j, :], in_=result[:])
 
-        basis_codes = {}
-        ahead = scalar_stage(0)
-        minus_outer = make_minus_outer(ahead[0], ahead[1])
-        for j in range(ROW_TILES):
-            nearest, inner_sq = ahead[2], ahead[3]
-            units = range(j * UNITS_PER_ROW_TILE, min((j + 1) * UNITS_PER_ROW_TILE, WEIGHT_UNITS))
-            grouped = [turn_unit(unit) for unit in units]
-            if j + 1 < ROW_TILES:
-                ahead = scalar_stage(j + 1)
+        def multiply_last(j):
+            halves = [slice(0, OUTS // 2), slice(OUTS // 2, OUTS)]
+            accs = []
+            for outs in halves:
+                acc = sums.tile([P, OUTS], F32, name="acc")
+                x_pass(acc, outs, j)
+                spline_passes(acc, outs, j, range(FOLDS))
+                accs.append(acc)
+            result = results.tile([P, OUTS], F32, name="result")
+            for acc, outs in zip(accs, halves):
+                spline_passes(acc, outs, j, range(FOLDS, SPLINES))
+            nc.vector.tensor_copy(out=result[:, halves[0]], in_=accs[0][:, halves[0]])
+            nc.sync.dma_start(out=out_rows[:, j, halves[0]], in_=result[:, halves[0]])
+            nc.scalar.copy(out=result[:, halves[1]], in_=accs[1][:, halves[1]])
+            nc.scalar.dma_start(out=out_rows[:, j, halves[1]], in_=result[:, halves[1]])
 
-            shifted = scratch.tile([P, 2, TILE_COLS], F32)
-            nc.vector.tensor_scalar(
-                out=shifted[:], in0=nearest[:], scalar1=0.5, scalar2=ROOT, op0=ALU.mult, op1=ALU.add
-            )
-            x_tile = x_turned[:, j, :, :].rearrange("p b t -> p (b t)")
-            below = scratch.tile([P, FOLDS, TILE_COLS], BF16)
-            for r in range(FOLDS):
-                nc.vector.tensor_scalar(
-                    out=below[:, r, :], in0=x_tile, scalar1=(r - 1.5) / 2.5, scalar2=None, op0=ALU.is_lt
-                )
-            inner = scratch.tile([P, 2, TILE_COLS], BF16)
+        pieces = []
+        for j in range(ROW_TILES):
+            cuts = [0, TILE_COLS // 2, TILE_COLS] if j in (0, ROW_TILES - 1) else [0, TILE_COLS]
+            for k in range(len(cuts) - 1):
+                pieces.append((j, slice(cuts[k], cuts[k + 1]), k == 0, k == len(cuts) - 2))
+        scalar_out = {}
+
+        def scalar_tile(tile):
+            scalar_out[tile] = scalar_tiles()
+            for j, cols, first, last in pieces:
+                if j == tile:
+                    scalar_stage(j, cols, scalar_out[j])
+
+        minus_outers = {}
+
+        def outer_piece(n):
+            j, cols, first, last = pieces[n]
+            if first:
+                minus_outers[j] = scratch.tile([P, FOLDS, TILE_COLS], BF16, name="minus_outer")
             nc.vector.scalar_tensor_tensor(
-                out=inner[:], in0=inner_sq[:], scalar=REST, in1=shifted[:], op0=ALU.add, op1=ALU.mult
+                out=minus_outers[j][:, :, cols],
+                in0=scalar_out[j][0][:, :, cols],
+                scalar=1.0,
+                in1=scalar_out[j][1][:, :, cols],
+                op0=ALU.subtract,
+                op1=ALU.mult,
             )
-            outer = scratch.tile([P, FOLDS, TILE_COLS], BF16)
+
+        scalar_tile(0)
+        outer_piece(0)
+        for n in range(len(pieces)):
+            j, cols, first, last = pieces[n]
+            nearest, inner_sq = scalar_out[j][2], scalar_out[j][3]
+            width = cols.stop - cols.start
+            if first:
+                units = range(j * UNITS_PER_ROW_TILE, min((j + 1) * UNITS_PER_ROW_TILE, WEIGHT_UNITS))
+                grouped = [turn_unit(unit) for unit in units]
+                shifted = scratch.tile([P, 2, TILE_COLS], F32)
+                below = scratch.tile([P, FOLDS, TILE_COLS], BF16)
+                inner = scratch.tile([P, 2, TILE_COLS], BF16)
+                outer = scratch.tile([P, FOLDS, TILE_COLS], BF16)
+                value = scratch.tile([P, FOLDS, TILE_COLS], BF16)
+                if j > 0:
+                    done_low, done_high = low, high
+                low = work.tile([P, FOLDS, TILE_COLS], BF16, align_bytes=64)
+                high = work.tile([P, FOLDS, TILE_COLS], BF16, align_bytes=64)
+                if j + 1 < ROW_TILES:
+                    scalar_tile(j + 1)
+
             nc.vector.tensor_scalar(
-                out=outer[:], in0=minus_outer[:], scalar1=-1.0, scalar2=0.0, op0=ALU.mult, op1=ALU.max
+                out=shifted[:, :, cols], in0=nearest[:, :, cols], scalar1=0.5, scalar2=ROOT, op0=ALU.mult, op1=ALU.add
             )
-            if j > 0:
-                quantise_splines(low, b_codes, b_scales, 0)
-            value = scratch.tile([P, FOLDS, TILE_COLS], BF16)
+            nc.vector.tensor_scalar(
+                out=outer[:, :, cols], in0=minus_outers[j][:, :, cols], scalar1=-1.0, scalar2=0.0, op0=ALU.mult, op1=ALU.max
+            )
+            nc.vector.scalar_tensor_tensor(
+                out=inner[:, :, cols],
+                in0=inner_sq[:, :, cols],
+                scalar=REST,
+                in1=shifted[:, :, cols],
+                op0=ALU.add,
+                op1=ALU.mult,
+            )
+            if first:
+                x_tile = x_turned[:, j, :, :].rearrange("p b t -> p (b t)")
+                for r in range(FOLDS):
+                    nc.vector.tensor_scalar(
+                        out=below[:, r, :], in0=x_tile, scalar1=(r - 1.5) / 2.5, scalar2=None, op0=ALU.is_lt
+                    )
+                if j > 0:
+                    quantise_splines(done_low, b_codes, b_scales, 0)
             nc.vector.tensor_tensor(
-                out=value[:].rearrange("p (h g) c -> p h (g c)", g=2),
-                in0=outer[:].rearrange("p (h g) c -> p h (g c)", g=2),
-                in1=inner[:].rearrange("p g c -> p (g c)").unsqueeze(1).to_broadcast([P, 2, 2 * TILE_COLS]),
+                out=value[:, :, cols].rearrange("p (h g) c -> p h g c", g=2),
+                in0=outer[:, :, cols].rearrange("p (h g) c -> p h g c", g=2),
+                in1=inner[:, :, cols].unsqueeze(1).to_broadcast([P, 2, 2, width]),
                 op=ALU.min,
             )
-            if j > 0:
-                quantise_splines(high, b_codes, b_scales, FOLDS)
-            for unit, w_grouped in zip(units, grouped):
-                quantise_unit(unit, w_grouped)
-            low = work.tile([P, FOLDS, TILE_COLS], BF16, align_bytes=64)
-            nc.vector.tensor_tensor(out=low[:], in0=value[:], in1=below[:], op=ALU.mult)
-            if j + 1 < ROW_TILES:
-                minus_outer = make_minus_outer(ahead[0], ahead[1])
-            high = work.tile([P, FOLDS, TILE_COLS], BF16, align_bytes=64)
-            nc.vector.tensor_tensor(out=high[:], in0=value[:], in1=low[:], op=ALU.subtract)
-            b_codes = codes.tile([P, SPLINES, P], U32, align_bytes=64)
-            b_scales = codes.tile([P, SPLINES, P], U8, align_bytes=64)
-            basis_codes[j] = (b_codes, b_scales)
-
-            if j >= MULTIPLY_LAG:
-                multiply(j - MULTIPLY_LAG, basis_codes[j - MULTIPLY_LAG][0], basis_codes[j - MULTIPLY_LAG][1])
+            if first and j > 0:
+                quantise_splines(done_high, b_codes, b_scales, FOLDS)
+            if last:
+                for unit, w_grouped in zip(units, grouped):
+                    quantise_unit(unit, w_grouped)
+            nc.vector.tensor_tensor(
+                out=low[:, :, cols], in0=value[:, :, cols], in1=below[:, :, cols], op=ALU.mult
+            )
+            if n + 1 < len(pieces):
+                outer_piece(n + 1)
+            nc.vector.tensor_tensor(
+                out=high[:, :, cols], in0=value[:, :, cols], in1=low[:, :, cols], op=ALU.subtract
+            )
+            if last:
+                b_codes = codes.tile([P, SPLINES, P], U32, align_bytes=64)
+                b_scales = codes.tile([P, SPLINES, P], U8, align_bytes=64)
+                basis_codes[j] = (b_codes, b_scales)
+                if j >= MULTIPLY_LAG:
+                    multiply(j - MULTIPLY_LAG)
 
         quantise_splines(low, b_codes, b_scales, 0)
         quantise_splines(high, b_codes, b_scales, FOLDS)
-        for j in range(ROW_TILES - MULTIPLY_LAG, ROW_TILES):
-            multiply(j, basis_codes[j][0], basis_codes[j][1])
+        for j in range(ROW_TILES - MULTIPLY_LAG, ROW_TILES - 1):
+            multiply(j)
+        multiply_last(ROW_TILES - 1)

@@ -23,11 +23,12 @@ FOLDS = SPLINES // 2
 ROW_TILES = BATCH // P
 OUT_TILES = OUTS // P
 TILE_COLS = P * PACK
-WORDS_PER_FEATURE = SPLINES // 2
-WEIGHT_UNITS = OUT_TILES * WORDS_PER_FEATURE
-UNITS_PER_ROW_TILE = 3
-VECTOR_UNITS = 4
-MULTIPLY_LAG = (WEIGHT_UNITS - 1) // UNITS_PER_ROW_TILE
+SPLINE_PAIRS = SPLINES // 2
+WEIGHT_UNITS = OUT_TILES * SPLINE_PAIRS
+GROUP = P // PACK
+UNITS_PER_ROW_TILE = 4
+WEIGHTS_DONE = (WEIGHT_UNITS - 1) // UNITS_PER_ROW_TILE
+X_PAIRS = {1: (0,), 2: (1,), 3: (2, 3)}
 ROOT = (2.0 ** (1.0 / 3.0) + 2.0 ** (-1.0 / 3.0) - 1.0) / 3.0
 REST = 4.0 * (ROOT * ROOT + ROOT) - (1.0 + ROOT) ** 2
 
@@ -41,7 +42,7 @@ def tile_kanlayer_kernel(tc, x, base_weight_words, base_weight_scales, spline_we
         weight_stage = ctx.enter_context(tc.tile_pool(name="weight_stage", bufs=2 * UNITS_PER_ROW_TILE))
         work = ctx.enter_context(tc.tile_pool(name="work", bufs=2))
         scratch = ctx.enter_context(tc.tile_pool(name="scratch", bufs=1))
-        codes = ctx.enter_context(tc.tile_pool(name="codes", bufs=MULTIPLY_LAG + 2))
+        codes = ctx.enter_context(tc.tile_pool(name="codes", bufs=WEIGHTS_DONE + 2))
         results = ctx.enter_context(tc.tile_pool(name="results", bufs=3))
         turned = ctx.enter_context(tc.psum_pool(name="turned", bufs=4))
         sums = ctx.enter_context(tc.psum_pool(name="sums", bufs=3))
@@ -49,18 +50,27 @@ def tile_kanlayer_kernel(tc, x, base_weight_words, base_weight_scales, spline_we
 
         ident = keep.tile([P, P], F32)
         make_identity(nc, ident[:])
+        ident_bf16 = keep.tile([P, P], BF16)
+        make_identity(nc, ident_bf16[:])
         base_scales = keep.tile([P, OUTS], U8, align_bytes=64)
         nc.vector.memset(base_scales[:].bitcast(I32), 0)
 
-        x_rows = x.rearrange("(p j) i -> p j i", j=ROW_TILES)
-        out_rows = out.rearrange("(p j) o -> p j o", j=ROW_TILES)
-        x_sb = keep.tile([P, ROW_TILES, FEATURES], BF16)
-        for j in range(0, ROW_TILES, 2):
-            nc.sync.dma_start(out=x_sb[:, j : j + 2, :], in_=x_rows[:, j : j + 2, :])
-        w_rows = spline_weight.rearrange("(c p) i l -> p c (i l)", p=P)
-        w_sb = keep.tile([P, OUT_TILES, FEATURES * SPLINES], BF16)
+        x_runs = x.rearrange("b (t p) -> (b t) p", t=PACK).rearrange("(g q) p -> q g p", q=P)
+        x_run_sb = keep.tile([P, BATCH // GROUP, P], BF16)
+        groups_per_tile = P // GROUP
+        for first, count in ((0, 1), (1, 1), (2, 2), (4, 4)):
+            groups = slice(first * groups_per_tile, (first + count) * groups_per_tile)
+            nc.sync.dma_start(out=x_run_sb[:, groups, :], in_=x_runs[:, groups, :])
+        w_runs = spline_weight.rearrange("o (t p) l -> (o t) (p l)", t=PACK).rearrange("(g q) f -> q g f", q=P)
+        w_sb = keep.tile([P, OUTS // GROUP, P, SPLINES], BF16)
         for c in range(OUT_TILES):
-            nc.sync.dma_start(out=w_sb[:, c, :], in_=w_rows[:, c, :])
+            groups = slice(c * groups_per_tile, (c + 1) * groups_per_tile)
+            nc.sync.dma_start(
+                out=w_sb[:, groups, :, :].rearrange("q g p l -> q g (p l)"), in_=w_runs[:, groups, :]
+            )
+        x_sb = keep.tile([P, ROW_TILES, FEATURES], BF16)
+        nc.sync.dma_start(out=x_sb[:], in_=x.rearrange("(j p) i -> p j i", p=P))
+        out_rows = out.rearrange("(j p) o -> p j o", p=P)
         base_codes = keep.tile([P, OUTS], U32, align_bytes=64)
         nc.sync.dma_start(
             out=base_codes[:].bitcast(I32),
@@ -72,47 +82,62 @@ def tile_kanlayer_kernel(tc, x, base_weight_words, base_weight_scales, spline_we
                 in_=base_weight_scales[0, 4 * quadrant : 4 * quadrant + 4, :].bitcast(I32),
             )
 
-        x_words = x_sb[:].bitcast(F32)
         x_turned = keep.tile([P, ROW_TILES, P, PACK], BF16, align_bytes=64)
-        x_turned_words = x_turned[:].bitcast(F32)
-        for j in range(0, ROW_TILES, 2):
-            xt = turned.tile([P, 2, 2, P], F32, tag="turned")
-            for k in range(2):
-                for u in range(2):
-                    nc.tensor.transpose(xt[:, k, u, :], x_words[:, j + k, u : FEATURES // 2 : 2], ident[:])
-            nc.vector.tensor_copy(out=x_turned_words[:, j : j + 2, :, :], in_=xt[:].rearrange("p k u b -> p k b u"))
+
+        def turn_x(first, count):
+            xt = turned.tile([P, 2 * groups_per_tile, P], BF16, tag="turned", name="xt")
+            for k in range(count * groups_per_tile):
+                nc.tensor.transpose(xt[:, k, :], x_run_sb[:, first * groups_per_tile + k, :], ident_bf16[:])
+            nc.vector.tensor_copy(
+                out=x_turned[:, first : first + count, :, :].rearrange("p j b t -> p (j b t)"),
+                in_=xt[:, : count * groups_per_tile, :].rearrange("p k c -> p (k c)"),
+            )
+
+        turn_x(0, 1)
+        turn_x(1, 1)
+        for j in range(2, ROW_TILES, 2):
+            turn_x(j, 2)
 
         x_codes = keep.tile([P, ROW_TILES * P], U32, align_bytes=64)
         x_scales = keep.tile([P, ROW_TILES * P], U8, align_bytes=64)
-        nc.vector.quantize_mx(
-            out=x_codes[:].bitcast(FP8X4),
-            scales=x_scales[:],
-            in_=x_turned[:].rearrange("p j b t -> p (j b t)"),
-        )
+        x_grouped = keep.tile([P, ROW_TILES, P, PACK], BF16, align_bytes=64)
 
-        w_words = w_sb[:].bitcast(F32)
-        words_in_row = FEATURES * WORDS_PER_FEATURE
+        def turn_x_rows(j):
+            x_words = x_sb[:].bitcast(F32)
+            xt = turned.tile([P, 2, 2, P], F32, tag="turned", name="xt")
+            for k in range(2):
+                for u in range(2):
+                    nc.tensor.transpose(xt[:, k, u, :], x_words[:, j + k, u : FEATURES // 2 : 2], ident[:])
+            nc.scalar.copy(
+                out=x_grouped[:].bitcast(F32)[:, j : j + 2, :, :], in_=xt[:].rearrange("p k u b -> p k b u")
+            )
+
+        def quantise_x():
+            nc.vector.quantize_mx(
+                out=x_codes[:].bitcast(FP8X4),
+                scales=x_scales[:],
+                in_=x_grouped[:].rearrange("p j b t -> p (j b t)"),
+            )
+
         w_codes = keep.tile([P, SPLINES, OUTS], U32, align_bytes=64)
         w_scales = keep.tile([P, SPLINES, OUTS], U8, align_bytes=64)
 
         def turn_unit(unit):
-            c, w = divmod(unit, WORDS_PER_FEATURE)
-            wt = turned.tile([P, PACK, P], F32, tag="turned")
-            for t in range(PACK):
-                first_word = WORDS_PER_FEATURE * t + w
-                nc.tensor.transpose(
-                    wt[:, t, :], w_words[:, c, first_word : words_in_row : WORDS_PER_FEATURE * PACK], ident[:]
-                )
-            w_grouped = weight_stage.tile([P, 2, P, PACK], BF16, align_bytes=64)
-            pairs = wt[:].bitcast(BF16).rearrange("p t (o e) -> p e o t", e=2)
-            if unit < VECTOR_UNITS:
-                nc.vector.tensor_copy(out=w_grouped[:], in_=pairs)
-            else:
-                nc.scalar.copy(out=w_grouped[:], in_=pairs)
+            c, w = divmod(unit, SPLINE_PAIRS)
+            wt = turned.tile([P, 2, groups_per_tile, P], BF16, tag="turned", name="wt")
+            for e in range(2):
+                for k in range(groups_per_tile):
+                    nc.tensor.transpose(
+                        wt[:, e, k, :], w_sb[:, c * groups_per_tile + k, :, 2 * w + e], ident_bf16[:]
+                    )
+            w_grouped = weight_stage.tile([P, 2, P, PACK], BF16, align_bytes=64, name="w_grouped")
+            nc.scalar.copy(
+                out=w_grouped[:].rearrange("p e o t -> p (e o t)"), in_=wt[:].rearrange("p e k c -> p (e k c)")
+            )
             return w_grouped
 
         def quantise_unit(unit, w_grouped):
-            c, w = divmod(unit, WORDS_PER_FEATURE)
+            c, w = divmod(unit, SPLINE_PAIRS)
             for e in range(2):
                 nc.vector.quantize_mx(
                     out=w_codes[:, 2 * w + e, c * P : (c + 1) * P].bitcast(FP8X4),
@@ -186,8 +211,11 @@ def tile_kanlayer_kernel(tc, x, base_weight_words, base_weight_scales, spline_we
             acc = sums.tile([P, OUTS], F32, name="acc")
             x_pass(acc, slice(0, OUTS), j)
             spline_passes(acc, slice(0, OUTS), j, range(SPLINES))
+            return acc
+
+        def store(j, acc):
             result = results.tile([P, OUTS], F32, name="result")
-            nc.scalar.copy(out=result[:], in_=acc[:])
+            nc.vector.tensor_copy(out=result[:], in_=acc[:])
             nc.sync.dma_start(out=out_rows[:, j, :], in_=result[:])
 
         def multiply_last(j):
@@ -234,6 +262,8 @@ def tile_kanlayer_kernel(tc, x, base_weight_words, base_weight_scales, spline_we
                 op1=ALU.mult,
             )
 
+        multiplied = 0
+        accs = []
         scalar_tile(0)
         outer_piece(0)
         for n in range(len(pieces)):
@@ -252,6 +282,8 @@ def tile_kanlayer_kernel(tc, x, base_weight_words, base_weight_scales, spline_we
                     done_low, done_high = low, high
                 low = work.tile([P, FOLDS, TILE_COLS], BF16, align_bytes=64)
                 high = work.tile([P, FOLDS, TILE_COLS], BF16, align_bytes=64)
+                for pair in X_PAIRS.get(j, ()):
+                    turn_x_rows(2 * pair)
                 if j + 1 < ROW_TILES:
                     scalar_tile(j + 1)
 
@@ -269,6 +301,9 @@ def tile_kanlayer_kernel(tc, x, base_weight_words, base_weight_scales, spline_we
                 op0=ALU.add,
                 op1=ALU.mult,
             )
+            for row_tile, acc in accs:
+                store(row_tile, acc)
+            accs = []
             if first:
                 x_tile = x_turned[:, j, :, :].rearrange("p b t -> p (b t)")
                 for r in range(FOLDS):
@@ -285,6 +320,11 @@ def tile_kanlayer_kernel(tc, x, base_weight_words, base_weight_scales, spline_we
             )
             if first and j > 0:
                 quantise_splines(done_high, b_codes, b_scales, FOLDS)
+            if first and j == WEIGHTS_DONE + 1:
+                quantise_x()
+            while first and j > WEIGHTS_DONE and multiplied < j and len(accs) < 2:
+                accs.append((multiplied, multiply(multiplied)))
+                multiplied += 1
             if last:
                 for unit, w_grouped in zip(units, grouped):
                     quantise_unit(unit, w_grouped)
@@ -300,11 +340,7 @@ def tile_kanlayer_kernel(tc, x, base_weight_words, base_weight_scales, spline_we
                 b_codes = codes.tile([P, SPLINES, P], U32, align_bytes=64)
                 b_scales = codes.tile([P, SPLINES, P], U8, align_bytes=64)
                 basis_codes[j] = (b_codes, b_scales)
-                if j >= MULTIPLY_LAG:
-                    multiply(j - MULTIPLY_LAG)
 
         quantise_splines(low, b_codes, b_scales, 0)
         quantise_splines(high, b_codes, b_scales, FOLDS)
-        for j in range(ROW_TILES - MULTIPLY_LAG, ROW_TILES - 1):
-            multiply(j)
         multiply_last(ROW_TILES - 1)

@@ -265,33 +265,44 @@ def tile_kanlayer_kernel(tc, x, base_weight_words, base_weight_scales, spline_we
         multiplied = 0
         accs = []
         scalar_tile(0)
-        outer_piece(0)
         for n in range(len(pieces)):
             j, cols, first, last = pieces[n]
-            nearest, inner_sq = scalar_out[j][2], scalar_out[j][3]
+            half_s, outer_sq, nearest, inner_sq = scalar_out[j]
             width = cols.stop - cols.start
             if first:
                 units = range(j * UNITS_PER_ROW_TILE, min((j + 1) * UNITS_PER_ROW_TILE, WEIGHT_UNITS))
                 grouped = [turn_unit(unit) for unit in units]
+                minus_outer = scratch.tile([P, FOLDS, TILE_COLS], BF16)
                 shifted = scratch.tile([P, 2, TILE_COLS], F32)
                 below = scratch.tile([P, FOLDS, TILE_COLS], BF16)
                 inner = scratch.tile([P, 2, TILE_COLS], BF16)
                 outer = scratch.tile([P, FOLDS, TILE_COLS], BF16)
                 value = scratch.tile([P, FOLDS, TILE_COLS], BF16)
-                if j > 0:
-                    done_low, done_high = low, high
                 low = work.tile([P, FOLDS, TILE_COLS], BF16, align_bytes=64)
                 high = work.tile([P, FOLDS, TILE_COLS], BF16, align_bytes=64)
                 for pair in X_PAIRS.get(j, ()):
                     turn_x_rows(2 * pair)
                 if j + 1 < ROW_TILES:
                     scalar_tile(j + 1)
+                x_tile = x_turned[:, j, :, :].rearrange("p b t -> p (b t)")
+                for r in range(FOLDS):
+                    nc.vector.tensor_scalar(
+                        out=below[:, r, :], in0=x_tile, scalar1=(r - 1.5) / 2.5, scalar2=None, op0=ALU.is_lt
+                    )
 
+            nc.vector.scalar_tensor_tensor(
+                out=minus_outer[:, :, cols],
+                in0=half_s[:, :, cols],
+                scalar=1.0,
+                in1=outer_sq[:, :, cols],
+                op0=ALU.subtract,
+                op1=ALU.mult,
+            )
             nc.vector.tensor_scalar(
                 out=shifted[:, :, cols], in0=nearest[:, :, cols], scalar1=0.5, scalar2=ROOT, op0=ALU.mult, op1=ALU.add
             )
             nc.vector.tensor_scalar(
-                out=outer[:, :, cols], in0=minus_outers[j][:, :, cols], scalar1=-1.0, scalar2=0.0, op0=ALU.mult, op1=ALU.max
+                out=outer[:, :, cols], in0=minus_outer[:, :, cols], scalar1=-1.0, scalar2=0.0, op0=ALU.mult, op1=ALU.max
             )
             nc.vector.scalar_tensor_tensor(
                 out=inner[:, :, cols],
@@ -304,35 +315,20 @@ def tile_kanlayer_kernel(tc, x, base_weight_words, base_weight_scales, spline_we
             for row_tile, acc in accs:
                 store(row_tile, acc)
             accs = []
-            if first:
-                x_tile = x_turned[:, j, :, :].rearrange("p b t -> p (b t)")
-                for r in range(FOLDS):
-                    nc.vector.tensor_scalar(
-                        out=below[:, r, :], in0=x_tile, scalar1=(r - 1.5) / 2.5, scalar2=None, op0=ALU.is_lt
-                    )
-                if j > 0:
-                    quantise_splines(done_low, b_codes, b_scales, 0)
             nc.vector.tensor_tensor(
                 out=value[:, :, cols].rearrange("p (h g) c -> p h g c", g=2),
                 in0=outer[:, :, cols].rearrange("p (h g) c -> p h g c", g=2),
                 in1=inner[:, :, cols].unsqueeze(1).to_broadcast([P, 2, 2, width]),
                 op=ALU.min,
             )
-            if first and j > 0:
-                quantise_splines(done_high, b_codes, b_scales, FOLDS)
-            if first and j == WEIGHTS_DONE + 1:
-                quantise_x()
-            while first and j > WEIGHTS_DONE and multiplied < j and len(accs) < 2:
-                accs.append((multiplied, multiply(multiplied)))
-                multiplied += 1
-            if last:
-                for unit, w_grouped in zip(units, grouped):
-                    quantise_unit(unit, w_grouped)
+            ready = list(zip(units, grouped)) if last else []
+            for unit, w_grouped in ready[: len(ready) // 2]:
+                quantise_unit(unit, w_grouped)
             nc.vector.tensor_tensor(
                 out=low[:, :, cols], in0=value[:, :, cols], in1=below[:, :, cols], op=ALU.mult
             )
-            if n + 1 < len(pieces):
-                outer_piece(n + 1)
+            for unit, w_grouped in ready[len(ready) // 2 :]:
+                quantise_unit(unit, w_grouped)
             nc.vector.tensor_tensor(
                 out=high[:, :, cols], in0=value[:, :, cols], in1=low[:, :, cols], op=ALU.subtract
             )
@@ -340,7 +336,12 @@ def tile_kanlayer_kernel(tc, x, base_weight_words, base_weight_scales, spline_we
                 b_codes = codes.tile([P, SPLINES, P], U32, align_bytes=64)
                 b_scales = codes.tile([P, SPLINES, P], U8, align_bytes=64)
                 basis_codes[j] = (b_codes, b_scales)
+                quantise_splines(low, b_codes, b_scales, 0)
+                if j == WEIGHTS_DONE:
+                    quantise_x()
+                quantise_splines(high, b_codes, b_scales, FOLDS)
+                while WEIGHTS_DONE <= j < ROW_TILES - 1 and multiplied <= j and len(accs) < 2:
+                    accs.append((multiplied, multiply(multiplied)))
+                    multiplied += 1
 
-        quantise_splines(low, b_codes, b_scales, 0)
-        quantise_splines(high, b_codes, b_scales, FOLDS)
         multiply_last(ROW_TILES - 1)

@@ -1,3 +1,4 @@
+import functools
 import math
 from contextlib import ExitStack
 
@@ -26,9 +27,9 @@ TILE_COLS = P * PACK
 SPLINE_PAIRS = SPLINES // 2
 WEIGHT_UNITS = OUT_TILES * SPLINE_PAIRS
 GROUP = P // PACK
-UNITS_PER_ROW_TILE = 4
-WEIGHTS_DONE = (WEIGHT_UNITS - 1) // UNITS_PER_ROW_TILE
-X_PAIRS = {1: (0,), 2: (1,), 3: (2, 3)}
+UNITS_PER_ROW_TILE = 3
+FIRST_UNITS = 4
+WEIGHTS_DONE = 4
 ROOT = (2.0 ** (1.0 / 3.0) + 2.0 ** (-1.0 / 3.0) - 1.0) / 3.0
 REST = 4.0 * (ROOT * ROOT + ROOT) - (1.0 + ROOT) ** 2
 
@@ -39,12 +40,13 @@ def tile_kanlayer_kernel(tc, x, base_weight_words, base_weight_scales, spline_we
     nc = tc.nc
     with ExitStack() as ctx:
         keep = ctx.enter_context(tc.tile_pool(name="keep", bufs=1))
-        weight_stage = ctx.enter_context(tc.tile_pool(name="weight_stage", bufs=2 * UNITS_PER_ROW_TILE))
+        weight_stage = ctx.enter_context(tc.tile_pool(name="weight_stage", bufs=FIRST_UNITS + UNITS_PER_ROW_TILE))
         work = ctx.enter_context(tc.tile_pool(name="work", bufs=2))
         scratch = ctx.enter_context(tc.tile_pool(name="scratch", bufs=1))
         codes = ctx.enter_context(tc.tile_pool(name="codes", bufs=WEIGHTS_DONE + 2))
-        results = ctx.enter_context(tc.tile_pool(name="results", bufs=3))
+        results = ctx.enter_context(tc.tile_pool(name="results", bufs=4))
         turned = ctx.enter_context(tc.psum_pool(name="turned", bufs=4))
+        turned_x = ctx.enter_context(tc.psum_pool(name="turned_x", bufs=1))
         sums = ctx.enter_context(tc.psum_pool(name="sums", bufs=3))
         ctx.enter_context(tc.manual_schedule())
 
@@ -58,16 +60,26 @@ def tile_kanlayer_kernel(tc, x, base_weight_words, base_weight_scales, spline_we
         x_runs = x.rearrange("b (t p) -> (b t) p", t=PACK).rearrange("(g q) p -> q g p", q=P)
         x_run_sb = keep.tile([P, BATCH // GROUP, P], BF16)
         groups_per_tile = P // GROUP
-        for first, count in ((0, 1), (1, 1), (2, 2), (4, 4)):
+
+        def load_x_runs(first, count):
             groups = slice(first * groups_per_tile, (first + count) * groups_per_tile)
             nc.sync.dma_start(out=x_run_sb[:, groups, :], in_=x_runs[:, groups, :])
+
         w_runs = spline_weight.rearrange("o (t p) l -> (o t) (p l)", t=PACK).rearrange("(g q) f -> q g f", q=P)
         w_sb = keep.tile([P, OUTS // GROUP, P, SPLINES], BF16)
-        for c in range(OUT_TILES):
+
+        def load_w_runs(c):
             groups = slice(c * groups_per_tile, (c + 1) * groups_per_tile)
             nc.sync.dma_start(
                 out=w_sb[:, groups, :, :].rearrange("q g p l -> q g (p l)"), in_=w_runs[:, groups, :]
             )
+
+        load_x_runs(0, 1)
+        load_x_runs(1, 1)
+        load_w_runs(0)
+        load_x_runs(2, ROW_TILES - 2)
+        for c in range(1, OUT_TILES):
+            load_w_runs(c)
         x_sb = keep.tile([P, ROW_TILES, FEATURES], BF16)
         nc.sync.dma_start(out=x_sb[:], in_=x.rearrange("(j p) i -> p j i", p=P))
         out_rows = out.rearrange("(j p) o -> p j o", p=P)
@@ -85,18 +97,19 @@ def tile_kanlayer_kernel(tc, x, base_weight_words, base_weight_scales, spline_we
         x_turned = keep.tile([P, ROW_TILES, P, PACK], BF16, align_bytes=64)
 
         def turn_x(first, count):
-            xt = turned.tile([P, 2 * groups_per_tile, P], BF16, tag="turned", name="xt")
+            xt = turned_x.tile([P, 2 * groups_per_tile, P], BF16, name="xt_runs")
             for k in range(count * groups_per_tile):
                 nc.tensor.transpose(xt[:, k, :], x_run_sb[:, first * groups_per_tile + k, :], ident_bf16[:])
+            return xt
+
+        def take_x(first, count, xt):
             nc.vector.tensor_copy(
                 out=x_turned[:, first : first + count, :, :].rearrange("p j b t -> p (j b t)"),
                 in_=xt[:, : count * groups_per_tile, :].rearrange("p k c -> p (k c)"),
             )
 
-        turn_x(0, 1)
-        turn_x(1, 1)
-        for j in range(2, ROW_TILES, 2):
-            turn_x(j, 2)
+        for j in range(2):
+            take_x(j, 1, turn_x(j, 1))
 
         x_codes = keep.tile([P, ROW_TILES * P], U32, align_bytes=64)
         x_scales = keep.tile([P, ROW_TILES * P], U8, align_bytes=64)
@@ -108,6 +121,9 @@ def tile_kanlayer_kernel(tc, x, base_weight_words, base_weight_scales, spline_we
             for k in range(2):
                 for u in range(2):
                     nc.tensor.transpose(xt[:, k, u, :], x_words[:, j + k, u : FEATURES // 2 : 2], ident[:])
+            return xt
+
+        def take_x_rows(j, xt):
             nc.scalar.copy(
                 out=x_grouped[:].bitcast(F32)[:, j : j + 2, :, :], in_=xt[:].rearrange("p k u b -> p k b u")
             )
@@ -130,11 +146,12 @@ def tile_kanlayer_kernel(tc, x, base_weight_words, base_weight_scales, spline_we
                     nc.tensor.transpose(
                         wt[:, e, k, :], w_sb[:, c * groups_per_tile + k, :, 2 * w + e], ident_bf16[:]
                     )
-            w_grouped = weight_stage.tile([P, 2, P, PACK], BF16, align_bytes=64, name="w_grouped")
+            return wt
+
+        def take_unit(wt, w_grouped):
             nc.scalar.copy(
                 out=w_grouped[:].rearrange("p e o t -> p (e o t)"), in_=wt[:].rearrange("p e k c -> p (e k c)")
             )
-            return w_grouped
 
         def quantise_unit(unit, w_grouped):
             c, w = divmod(unit, SPLINE_PAIRS)
@@ -152,27 +169,42 @@ def tile_kanlayer_kernel(tc, x, base_weight_words, base_weight_scales, spline_we
             inner_sq = work.tile([P, 2, TILE_COLS], F32)
             return half_s, outer_sq, nearest, inner_sq
 
-        def scalar_stage(j, cols, tiles):
+        def scalar_stage(j, cols, tiles, copies):
             half_s, outer_sq, nearest, inner_sq = tiles
             x_tile = x_turned[:, j, :, :].rearrange("p b t -> p (b t)")[:, cols]
             for r in range(FOLDS):
                 nc.scalar.activation(
                     out=half_s[:, r, cols], in_=x_tile, func=ACT.Abs, scale=1.25, bias=(1.5 - r) / 2.0
                 )
-            nc.scalar.activation(out=half_s[:, :, cols], in_=half_s[:, :, cols], func=ACT.Abs, scale=1.0, bias=-1.0)
-            nc.scalar.activation(
-                out=outer_sq[:, :, cols],
-                in_=half_s[:, :, cols],
-                func=ACT.Square,
-                scale=math.sqrt(4.0 / 3.0),
-                bias=-math.sqrt(4.0 / 3.0),
-            )
+            pairs = (slice(0, 2), slice(2, 4))
+            for pair in pairs:
+                nc.scalar.activation(
+                    out=half_s[:, pair, cols], in_=half_s[:, pair, cols], func=ACT.Abs, scale=1.0, bias=-1.0
+                )
+                if copies:
+                    copies.pop(0)()
+
+            def square_outer(pair):
+                nc.scalar.activation(
+                    out=outer_sq[:, pair, cols],
+                    in_=half_s[:, pair, cols],
+                    func=ACT.Square,
+                    scale=math.sqrt(4.0 / 3.0),
+                    bias=-math.sqrt(4.0 / 3.0),
+                )
+
+            square_outer(pairs[0])
             nc.scalar.activation(
                 out=nearest[:, :, cols], in_=half_s[:, 1:3, cols], func=ACT.Abs, scale=2.0, bias=-1.0
             )
+            if copies:
+                copies.pop(0)()
+            square_outer(pairs[1])
             nc.scalar.activation(
                 out=inner_sq[:, :, cols], in_=nearest[:, :, cols], func=ACT.Square, scale=1.0, bias=-(1.0 + ROOT)
             )
+            if copies:
+                copies.pop(0)()
 
         def quantise_splines(four_splines, b_codes, b_scales, l0):
             nc.vector.quantize_mx(
@@ -215,7 +247,7 @@ def tile_kanlayer_kernel(tc, x, base_weight_words, base_weight_scales, spline_we
 
         def store(j, acc):
             result = results.tile([P, OUTS], F32, name="result")
-            nc.vector.tensor_copy(out=result[:], in_=acc[:])
+            nc.scalar.copy(out=result[:], in_=acc[:])
             nc.sync.dma_start(out=out_rows[:, j, :], in_=result[:])
 
         def multiply_last(j):
@@ -241,11 +273,11 @@ def tile_kanlayer_kernel(tc, x, base_weight_words, base_weight_scales, spline_we
                 pieces.append((j, slice(cuts[k], cuts[k + 1]), k == 0, k == len(cuts) - 2))
         scalar_out = {}
 
-        def scalar_tile(tile):
+        def scalar_tile(tile, copies):
             scalar_out[tile] = scalar_tiles()
             for j, cols, first, last in pieces:
                 if j == tile:
-                    scalar_stage(j, cols, scalar_out[j])
+                    scalar_stage(j, cols, scalar_out[j], copies)
 
         minus_outers = {}
 
@@ -264,14 +296,24 @@ def tile_kanlayer_kernel(tc, x, base_weight_words, base_weight_scales, spline_we
 
         multiplied = 0
         accs = []
-        scalar_tile(0)
+        staged = []
+        scalar_tile(0, [])
         for n in range(len(pieces)):
             j, cols, first, last = pieces[n]
             half_s, outer_sq, nearest, inner_sq = scalar_out[j]
             width = cols.stop - cols.start
             if first:
-                units = range(j * UNITS_PER_ROW_TILE, min((j + 1) * UNITS_PER_ROW_TILE, WEIGHT_UNITS))
-                grouped = [turn_unit(unit) for unit in units]
+                if 2 * j + 2 < ROW_TILES:
+                    xt = turn_x(2 * j + 2, 2)
+                next_unit = FIRST_UNITS + j * UNITS_PER_ROW_TILE
+                units = range(next_unit - UNITS_PER_ROW_TILE if j else 0, next_unit) if j <= WEIGHTS_DONE else range(0)
+                copies = []
+                done_units = staged
+                staged = []
+                for unit in units:
+                    w_grouped = weight_stage.tile([P, 2, P, PACK], BF16, align_bytes=64, name="w_grouped")
+                    copies.append(functools.partial(take_unit, turn_unit(unit), w_grouped))
+                    staged.append((unit, w_grouped))
                 minus_outer = scratch.tile([P, FOLDS, TILE_COLS], BF16)
                 shifted = scratch.tile([P, 2, TILE_COLS], F32)
                 below = scratch.tile([P, FOLDS, TILE_COLS], BF16)
@@ -280,30 +322,35 @@ def tile_kanlayer_kernel(tc, x, base_weight_words, base_weight_scales, spline_we
                 value = scratch.tile([P, FOLDS, TILE_COLS], BF16)
                 low = work.tile([P, FOLDS, TILE_COLS], BF16, align_bytes=64)
                 high = work.tile([P, FOLDS, TILE_COLS], BF16, align_bytes=64)
-                for pair in X_PAIRS.get(j, ()):
-                    turn_x_rows(2 * pair)
+                if 1 <= j <= ROW_TILES // 2:
+                    copies.append(functools.partial(take_x_rows, 2 * (j - 1), turn_x_rows(2 * (j - 1))))
+                for row_tile, acc in accs:
+                    store(row_tile, acc)
+                accs = []
+                if j == ROW_TILES - 2:
+                    accs = [(row_tile, multiply(row_tile)) for row_tile in (3, 4)]
                 if j + 1 < ROW_TILES:
-                    scalar_tile(j + 1)
-                x_tile = x_turned[:, j, :, :].rearrange("p b t -> p (b t)")
-                for r in range(FOLDS):
-                    nc.vector.tensor_scalar(
-                        out=below[:, r, :], in0=x_tile, scalar1=(r - 1.5) / 2.5, scalar2=None, op0=ALU.is_lt
-                    )
+                    scalar_tile(j + 1, copies)
 
-            nc.vector.scalar_tensor_tensor(
-                out=minus_outer[:, :, cols],
-                in0=half_s[:, :, cols],
-                scalar=1.0,
-                in1=outer_sq[:, :, cols],
-                op0=ALU.subtract,
-                op1=ALU.mult,
-            )
-            nc.vector.tensor_scalar(
-                out=shifted[:, :, cols], in0=nearest[:, :, cols], scalar1=0.5, scalar2=ROOT, op0=ALU.mult, op1=ALU.add
-            )
-            nc.vector.tensor_scalar(
-                out=outer[:, :, cols], in0=minus_outer[:, :, cols], scalar1=-1.0, scalar2=0.0, op0=ALU.mult, op1=ALU.max
-            )
+            pairs = (slice(0, 2), slice(2, 4))
+            for pair in pairs:
+                nc.vector.scalar_tensor_tensor(
+                    out=minus_outer[:, pair, cols],
+                    in0=half_s[:, pair, cols],
+                    scalar=1.0,
+                    in1=outer_sq[:, pair, cols],
+                    op0=ALU.subtract,
+                    op1=ALU.mult,
+                )
+                if pair.start == 0:
+                    nc.vector.tensor_scalar(
+                        out=shifted[:, :, cols],
+                        in0=nearest[:, :, cols],
+                        scalar1=0.5,
+                        scalar2=ROOT,
+                        op0=ALU.mult,
+                        op1=ALU.add,
+                    )
             nc.vector.scalar_tensor_tensor(
                 out=inner[:, :, cols],
                 in0=inner_sq[:, :, cols],
@@ -312,36 +359,46 @@ def tile_kanlayer_kernel(tc, x, base_weight_words, base_weight_scales, spline_we
                 op0=ALU.add,
                 op1=ALU.mult,
             )
-            for row_tile, acc in accs:
-                store(row_tile, acc)
-            accs = []
-            nc.vector.tensor_tensor(
-                out=value[:, :, cols].rearrange("p (h g) c -> p h g c", g=2),
-                in0=outer[:, :, cols].rearrange("p (h g) c -> p h g c", g=2),
-                in1=inner[:, :, cols].unsqueeze(1).to_broadcast([P, 2, 2, width]),
-                op=ALU.min,
+            nc.vector.tensor_scalar(
+                out=outer[:, :, cols], in0=minus_outer[:, :, cols], scalar1=-1.0, scalar2=0.0, op0=ALU.mult, op1=ALU.max
             )
-            ready = list(zip(units, grouped)) if last else []
-            for unit, w_grouped in ready[: len(ready) // 2]:
-                quantise_unit(unit, w_grouped)
-            nc.vector.tensor_tensor(
-                out=low[:, :, cols], in0=value[:, :, cols], in1=below[:, :, cols], op=ALU.mult
-            )
-            for unit, w_grouped in ready[len(ready) // 2 :]:
-                quantise_unit(unit, w_grouped)
-            nc.vector.tensor_tensor(
-                out=high[:, :, cols], in0=value[:, :, cols], in1=low[:, :, cols], op=ALU.subtract
-            )
+            if first:
+                x_tile = x_turned[:, j, :, :].rearrange("p b t -> p (b t)")
+                for unit, w_grouped in done_units:
+                    quantise_unit(unit, w_grouped)
+                if j == WEIGHTS_DONE + 1:
+                    quantise_x()
+                    for multiplied in range(3):
+                        accs.append((multiplied, multiply(multiplied)))
+                for r in range(FOLDS):
+                    nc.vector.tensor_scalar(
+                        out=below[:, r, :], in0=x_tile, scalar1=(r - 1.5) / 2.5, scalar2=None, op0=ALU.is_lt
+                    )
+            for pair in pairs:
+                nc.vector.tensor_tensor(
+                    out=value[:, pair, cols], in0=outer[:, pair, cols], in1=inner[:, :, cols], op=ALU.min
+                )
+            for pair in pairs:
+                nc.vector.tensor_tensor(
+                    out=low[:, pair, cols], in0=value[:, pair, cols], in1=below[:, pair, cols], op=ALU.mult
+                )
+            for pair in pairs:
+                nc.vector.tensor_tensor(
+                    out=high[:, pair, cols], in0=value[:, pair, cols], in1=low[:, pair, cols], op=ALU.subtract
+                )
             if last:
+                if 2 * j + 2 < ROW_TILES:
+                    take_x(2 * j + 2, 2, xt)
                 b_codes = codes.tile([P, SPLINES, P], U32, align_bytes=64)
                 b_scales = codes.tile([P, SPLINES, P], U8, align_bytes=64)
                 basis_codes[j] = (b_codes, b_scales)
                 quantise_splines(low, b_codes, b_scales, 0)
-                if j == WEIGHTS_DONE:
-                    quantise_x()
                 quantise_splines(high, b_codes, b_scales, FOLDS)
-                while WEIGHTS_DONE <= j < ROW_TILES - 1 and multiplied <= j and len(accs) < 2:
-                    accs.append((multiplied, multiply(multiplied)))
-                    multiplied += 1
+                if j == ROW_TILES - 2:
+                    for row_tile, acc in accs:
+                        store(row_tile, acc)
+                    accs = [(row_tile, multiply(row_tile)) for row_tile in (5, 6)]
 
+        for row_tile, acc in accs:
+            store(row_tile, acc)
         multiply_last(ROW_TILES - 1)

@@ -29,6 +29,9 @@ WEIGHT_UNITS = OUT_TILES * SPLINE_PAIRS
 GROUP = P // PACK
 UNITS_PER_ROW_TILE = 3
 FIRST_UNITS = 4
+MASK_BUFS = 5
+VECTOR_UNITS = tuple(range(FIRST_UNITS, FIRST_UNITS + 3 * UNITS_PER_ROW_TILE, UNITS_PER_ROW_TILE))
+MASKS_BEFORE = {1: (2, 3), 2: (4,), 3: (5,), 4: (6,), 5: (7,)}
 WEIGHTS_DONE = 4
 ROOT = (2.0 ** (1.0 / 3.0) + 2.0 ** (-1.0 / 3.0) - 1.0) / 3.0
 REST = 4.0 * (ROOT * ROOT + ROOT) - (1.0 + ROOT) ** 2
@@ -45,9 +48,10 @@ def tile_kanlayer_kernel(tc, x, base_weight_words, base_weight_scales, spline_we
         scratch = ctx.enter_context(tc.tile_pool(name="scratch", bufs=1))
         codes = ctx.enter_context(tc.tile_pool(name="codes", bufs=WEIGHTS_DONE + 2))
         results = ctx.enter_context(tc.tile_pool(name="results", bufs=4))
-        turned = ctx.enter_context(tc.psum_pool(name="turned", bufs=4))
-        turned_x = ctx.enter_context(tc.psum_pool(name="turned_x", bufs=1))
-        sums = ctx.enter_context(tc.psum_pool(name="sums", bufs=3))
+        mask_stage = ctx.enter_context(tc.tile_pool(name="mask_stage", bufs=MASK_BUFS))
+        turned_x = ctx.enter_context(tc.psum_pool(name="turned_x", bufs=2))
+        turned_masks = ctx.enter_context(tc.psum_pool(name="turned_masks", bufs=2))
+        banks = ctx.enter_context(tc.psum_pool(name="banks", bufs=4))
         ctx.enter_context(tc.manual_schedule())
 
         ident = keep.tile([P, P], F32)
@@ -76,8 +80,9 @@ def tile_kanlayer_kernel(tc, x, base_weight_words, base_weight_scales, spline_we
 
         load_x_runs(0, 1)
         load_x_runs(1, 1)
+        load_x_runs(2, 2)
         load_w_runs(0)
-        load_x_runs(2, ROW_TILES - 2)
+        load_x_runs(4, ROW_TILES - 4)
         for c in range(1, OUT_TILES):
             load_w_runs(c)
         x_sb = keep.tile([P, ROW_TILES, FEATURES], BF16)
@@ -94,22 +99,45 @@ def tile_kanlayer_kernel(tc, x, base_weight_words, base_weight_scales, spline_we
                 in_=base_weight_scales[0, 4 * quadrant : 4 * quadrant + 4, :].bitcast(I32),
             )
 
-        x_turned = keep.tile([P, ROW_TILES, P, PACK], BF16, align_bytes=64)
+        def groups_of(j):
+            return slice(j * groups_per_tile, (j + 1) * groups_per_tile)
 
-        def turn_x(first, count):
-            xt = turned_x.tile([P, 2 * groups_per_tile, P], BF16, name="xt_runs")
-            for k in range(count * groups_per_tile):
-                nc.tensor.transpose(xt[:, k, :], x_run_sb[:, first * groups_per_tile + k, :], ident_bf16[:])
-            return xt
+        x_banks = {}
 
-        def take_x(first, count, xt):
-            nc.vector.tensor_copy(
-                out=x_turned[:, first : first + count, :, :].rearrange("p j b t -> p (j b t)"),
-                in_=xt[:, : count * groups_per_tile, :].rearrange("p k c -> p (k c)"),
-            )
+        def turn_x(j):
+            x_bank = turned_x.tile([P, 2, groups_per_tile, P], BF16, name="x_bank")
+            x_banks[j] = x_bank[:, 0, :, :]
+            for k in range(groups_per_tile):
+                nc.tensor.transpose(x_bank[:, 0, k, :], x_run_sb[:, j * groups_per_tile + k, :], ident_bf16[:])
 
-        for j in range(2):
-            take_x(j, 1, turn_x(j, 1))
+        below_runs = {}
+        below_banks = {}
+
+        def make_masks(j):
+            below_runs[j] = mask_stage.tile([P, FOLDS, groups_per_tile, P], BF16, name="below_run")
+            for r in range(FOLDS):
+                nc.vector.tensor_scalar(
+                    out=below_runs[j][:, r, :, :],
+                    in0=x_run_sb[:, groups_of(j), :],
+                    scalar1=(r - 1.5) / 2.5,
+                    scalar2=None,
+                    op0=ALU.is_lt,
+                )
+
+        def turn_masks(j):
+            below_banks[j] = []
+            for first_fold in range(0, FOLDS, 2):
+                below_bank = turned_masks.tile([P, 2, groups_per_tile, P], BF16, name="below_bank")
+                for e in range(2):
+                    for k in range(groups_per_tile):
+                        nc.tensor.transpose(below_bank[:, e, k, :], below_runs[j][:, first_fold + e, k, :], ident_bf16[:])
+                below_banks[j].append(below_bank)
+
+        turn_x(0)
+        make_masks(0)
+        turn_x(1)
+        make_masks(1)
+        turn_masks(0)
 
         x_codes = keep.tile([P, ROW_TILES * P], U32, align_bytes=64)
         x_scales = keep.tile([P, ROW_TILES * P], U8, align_bytes=64)
@@ -117,7 +145,7 @@ def tile_kanlayer_kernel(tc, x, base_weight_words, base_weight_scales, spline_we
 
         def turn_x_rows(j):
             x_words = x_sb[:].bitcast(F32)
-            xt = turned.tile([P, 2, 2, P], F32, tag="turned", name="xt")
+            xt = banks.tile([P, 2, 2, P], F32, tag="bank", name="xt")
             for k in range(2):
                 for u in range(2):
                     nc.tensor.transpose(xt[:, k, u, :], x_words[:, j + k, u : FEATURES // 2 : 2], ident[:])
@@ -140,7 +168,7 @@ def tile_kanlayer_kernel(tc, x, base_weight_words, base_weight_scales, spline_we
 
         def turn_unit(unit):
             c, w = divmod(unit, SPLINE_PAIRS)
-            wt = turned.tile([P, 2, groups_per_tile, P], BF16, tag="turned", name="wt")
+            wt = banks.tile([P, 2, groups_per_tile, P], BF16, tag="bank", name="wt")
             for e in range(2):
                 for k in range(groups_per_tile):
                     nc.tensor.transpose(
@@ -148,10 +176,8 @@ def tile_kanlayer_kernel(tc, x, base_weight_words, base_weight_scales, spline_we
                     )
             return wt
 
-        def take_unit(wt, w_grouped):
-            nc.scalar.copy(
-                out=w_grouped[:].rearrange("p e o t -> p (e o t)"), in_=wt[:].rearrange("p e k c -> p (e k c)")
-            )
+        def take_unit(copy, wt, w_grouped):
+            copy(out=w_grouped[:].rearrange("p e o t -> p (e o t)"), in_=wt[:].rearrange("p e k c -> p (e k c)"))
 
         def quantise_unit(unit, w_grouped):
             c, w = divmod(unit, SPLINE_PAIRS)
@@ -171,7 +197,7 @@ def tile_kanlayer_kernel(tc, x, base_weight_words, base_weight_scales, spline_we
 
         def scalar_stage(j, cols, tiles, copies):
             half_s, outer_sq, nearest, inner_sq = tiles
-            x_tile = x_turned[:, j, :, :].rearrange("p b t -> p (b t)")[:, cols]
+            x_tile = x_banks[j].rearrange("p k c -> p (k c)")[:, cols]
             for r in range(FOLDS):
                 nc.scalar.activation(
                     out=half_s[:, r, cols], in_=x_tile, func=ACT.Abs, scale=1.25, bias=(1.5 - r) / 2.0
@@ -240,7 +266,7 @@ def tile_kanlayer_kernel(tc, x, base_weight_words, base_weight_scales, spline_we
                 )
 
         def multiply(j):
-            acc = sums.tile([P, OUTS], F32, name="acc")
+            acc = banks.tile([P, OUTS], F32, tag="bank", name="acc")
             x_pass(acc, slice(0, OUTS), j)
             spline_passes(acc, slice(0, OUTS), j, range(SPLINES))
             return acc
@@ -254,7 +280,7 @@ def tile_kanlayer_kernel(tc, x, base_weight_words, base_weight_scales, spline_we
             halves = [slice(0, OUTS // 2), slice(OUTS // 2, OUTS)]
             accs = []
             for outs in halves:
-                acc = sums.tile([P, OUTS], F32, name="acc")
+                acc = banks.tile([P, OUTS], F32, tag="bank", name="acc")
                 x_pass(acc, outs, j)
                 spline_passes(acc, outs, j, range(FOLDS))
                 accs.append(acc)
@@ -279,51 +305,39 @@ def tile_kanlayer_kernel(tc, x, base_weight_words, base_weight_scales, spline_we
                 if j == tile:
                     scalar_stage(j, cols, scalar_out[j], copies)
 
-        minus_outers = {}
-
-        def outer_piece(n):
-            j, cols, first, last = pieces[n]
-            if first:
-                minus_outers[j] = scratch.tile([P, FOLDS, TILE_COLS], BF16, name="minus_outer")
-            nc.vector.scalar_tensor_tensor(
-                out=minus_outers[j][:, :, cols],
-                in0=scalar_out[j][0][:, :, cols],
-                scalar=1.0,
-                in1=scalar_out[j][1][:, :, cols],
-                op0=ALU.subtract,
-                op1=ALU.mult,
-            )
-
-        multiplied = 0
         accs = []
         staged = []
         scalar_tile(0, [])
         for n in range(len(pieces)):
             j, cols, first, last = pieces[n]
             half_s, outer_sq, nearest, inner_sq = scalar_out[j]
-            width = cols.stop - cols.start
             if first:
-                if 2 * j + 2 < ROW_TILES:
-                    xt = turn_x(2 * j + 2, 2)
+                if j + 2 < ROW_TILES:
+                    turn_x(j + 2)
                 next_unit = FIRST_UNITS + j * UNITS_PER_ROW_TILE
                 units = range(next_unit - UNITS_PER_ROW_TILE if j else 0, next_unit) if j <= WEIGHTS_DONE else range(0)
                 copies = []
+                vector_copies = []
                 done_units = staged
                 staged = []
                 for unit in units:
                     w_grouped = weight_stage.tile([P, 2, P, PACK], BF16, align_bytes=64, name="w_grouped")
-                    copies.append(functools.partial(take_unit, turn_unit(unit), w_grouped))
+                    if unit in VECTOR_UNITS:
+                        vector_copies.append(functools.partial(take_unit, nc.vector.tensor_copy, turn_unit(unit), w_grouped))
+                    else:
+                        copies.append(functools.partial(take_unit, nc.scalar.copy, turn_unit(unit), w_grouped))
                     staged.append((unit, w_grouped))
                 minus_outer = scratch.tile([P, FOLDS, TILE_COLS], BF16)
                 shifted = scratch.tile([P, 2, TILE_COLS], F32)
-                below = scratch.tile([P, FOLDS, TILE_COLS], BF16)
                 inner = scratch.tile([P, 2, TILE_COLS], BF16)
                 outer = scratch.tile([P, FOLDS, TILE_COLS], BF16)
                 value = scratch.tile([P, FOLDS, TILE_COLS], BF16)
-                low = work.tile([P, FOLDS, TILE_COLS], BF16, align_bytes=64)
-                high = work.tile([P, FOLDS, TILE_COLS], BF16, align_bytes=64)
+                low = scratch.tile([P, FOLDS, TILE_COLS], BF16, align_bytes=64)
+                high = scratch.tile([P, FOLDS, TILE_COLS], BF16, align_bytes=64)
                 if 1 <= j <= ROW_TILES // 2:
                     copies.append(functools.partial(take_x_rows, 2 * (j - 1), turn_x_rows(2 * (j - 1))))
+                if 0 < j < ROW_TILES - 1:
+                    turn_masks(j)
                 for row_tile, acc in accs:
                     store(row_tile, acc)
                 accs = []
@@ -332,6 +346,11 @@ def tile_kanlayer_kernel(tc, x, base_weight_words, base_weight_scales, spline_we
                 if j + 1 < ROW_TILES:
                     scalar_tile(j + 1, copies)
 
+            for ahead in MASKS_BEFORE.get(n, ()):
+                make_masks(ahead)
+            for copy in vector_copies:
+                copy()
+            vector_copies = []
             pairs = (slice(0, 2), slice(2, 4))
             for pair in pairs:
                 nc.vector.scalar_tensor_tensor(
@@ -351,50 +370,54 @@ def tile_kanlayer_kernel(tc, x, base_weight_words, base_weight_scales, spline_we
                         op0=ALU.mult,
                         op1=ALU.add,
                     )
-            nc.vector.scalar_tensor_tensor(
-                out=inner[:, :, cols],
-                in0=inner_sq[:, :, cols],
-                scalar=REST,
-                in1=shifted[:, :, cols],
-                op0=ALU.add,
-                op1=ALU.mult,
-            )
-            nc.vector.tensor_scalar(
-                out=outer[:, :, cols], in0=minus_outer[:, :, cols], scalar1=-1.0, scalar2=0.0, op0=ALU.mult, op1=ALU.max
-            )
+            for pair in pairs:
+                nc.vector.tensor_scalar(
+                    out=outer[:, pair, cols],
+                    in0=minus_outer[:, pair, cols],
+                    scalar1=-1.0,
+                    scalar2=0.0,
+                    op0=ALU.mult,
+                    op1=ALU.max,
+                )
+                if pair.start == 0:
+                    nc.vector.scalar_tensor_tensor(
+                        out=inner[:, :, cols],
+                        in0=inner_sq[:, :, cols],
+                        scalar=REST,
+                        in1=shifted[:, :, cols],
+                        op0=ALU.add,
+                        op1=ALU.mult,
+                    )
             if first:
-                x_tile = x_turned[:, j, :, :].rearrange("p b t -> p (b t)")
                 for unit, w_grouped in done_units:
                     quantise_unit(unit, w_grouped)
                 if j == WEIGHTS_DONE + 1:
                     quantise_x()
                     for multiplied in range(3):
                         accs.append((multiplied, multiply(multiplied)))
-                for r in range(FOLDS):
-                    nc.vector.tensor_scalar(
-                        out=below[:, r, :], in0=x_tile, scalar1=(r - 1.5) / 2.5, scalar2=None, op0=ALU.is_lt
-                    )
             for pair in pairs:
                 nc.vector.tensor_tensor(
                     out=value[:, pair, cols], in0=outer[:, pair, cols], in1=inner[:, :, cols], op=ALU.min
                 )
-            for pair in pairs:
+            for pair, below_bank in zip(pairs, below_banks[j]):
                 nc.vector.tensor_tensor(
-                    out=low[:, pair, cols], in0=value[:, pair, cols], in1=below[:, pair, cols], op=ALU.mult
+                    out=low[:, pair, cols],
+                    in0=value[:, pair, cols],
+                    in1=below_bank[:].rearrange("p e k c -> p e (k c)")[:, :, cols],
+                    op=ALU.mult,
                 )
             for pair in pairs:
                 nc.vector.tensor_tensor(
                     out=high[:, pair, cols], in0=value[:, pair, cols], in1=low[:, pair, cols], op=ALU.subtract
                 )
             if last:
-                if 2 * j + 2 < ROW_TILES:
-                    take_x(2 * j + 2, 2, xt)
                 b_codes = codes.tile([P, SPLINES, P], U32, align_bytes=64)
                 b_scales = codes.tile([P, SPLINES, P], U8, align_bytes=64)
                 basis_codes[j] = (b_codes, b_scales)
                 quantise_splines(low, b_codes, b_scales, 0)
                 quantise_splines(high, b_codes, b_scales, FOLDS)
                 if j == ROW_TILES - 2:
+                    turn_masks(j + 1)
                     for row_tile, acc in accs:
                         store(row_tile, acc)
                     accs = [(row_tile, multiply(row_tile)) for row_tile in (5, 6)]

@@ -29,10 +29,10 @@ WEIGHT_UNITS = OUT_TILES * SPLINE_PAIRS
 GROUP = P // PACK
 UNITS_PER_ROW_TILE = 3
 FIRST_UNITS = 4
-MASK_BUFS = 5
-VECTOR_UNITS = tuple(range(FIRST_UNITS, FIRST_UNITS + 3 * UNITS_PER_ROW_TILE, UNITS_PER_ROW_TILE))
-MASKS_BEFORE = {1: (2, 3), 2: (4,), 3: (5,), 4: (6,), 5: (7,)}
+MASK_BUFS = 4
 WEIGHTS_DONE = 4
+CENTRED_FOLDS = 2
+SHIFTED_BY_SCALAR = range(WEIGHTS_DONE + 1, ROW_TILES)
 ROOT = (2.0 ** (1.0 / 3.0) + 2.0 ** (-1.0 / 3.0) - 1.0) / 3.0
 REST = 4.0 * (ROOT * ROOT + ROOT) - (1.0 + ROOT) ** 2
 
@@ -49,15 +49,20 @@ def tile_kanlayer_kernel(tc, x, base_weight_words, base_weight_scales, spline_we
         codes = ctx.enter_context(tc.tile_pool(name="codes", bufs=WEIGHTS_DONE + 2))
         results = ctx.enter_context(tc.tile_pool(name="results", bufs=4))
         mask_stage = ctx.enter_context(tc.tile_pool(name="mask_stage", bufs=MASK_BUFS))
-        turned_x = ctx.enter_context(tc.psum_pool(name="turned_x", bufs=2))
+        turned_x = ctx.enter_context(tc.psum_pool(name="turned_x", bufs=1))
+        centred = ctx.enter_context(tc.psum_pool(name="centred", bufs=CENTRED_FOLDS))
         turned_masks = ctx.enter_context(tc.psum_pool(name="turned_masks", bufs=2))
-        banks = ctx.enter_context(tc.psum_pool(name="banks", bufs=4))
+        banks = ctx.enter_context(tc.psum_pool(name="banks", bufs=3))
         ctx.enter_context(tc.manual_schedule())
 
         ident = keep.tile([P, P], F32)
         make_identity(nc, ident[:])
         ident_bf16 = keep.tile([P, P], BF16)
         make_identity(nc, ident_bf16[:])
+        turn_x_scaled = keep.tile([P, P], BF16)
+        nc.scalar.activation(out=turn_x_scaled[:], in_=ident_bf16[:], func=ACT.Copy, scale=1.25)
+        turn_mask_doubled = keep.tile([P, P], BF16)
+        nc.scalar.activation(out=turn_mask_doubled[:], in_=ident_bf16[:], func=ACT.Copy, scale=2.0)
         base_scales = keep.tile([P, OUTS], U8, align_bytes=64)
         nc.vector.memset(base_scales[:].bitcast(I32), 0)
 
@@ -133,10 +138,31 @@ def tile_kanlayer_kernel(tc, x, base_weight_words, base_weight_scales, spline_we
                         nc.tensor.transpose(below_bank[:, e, k, :], below_runs[j][:, first_fold + e, k, :], ident_bf16[:])
                 below_banks[j].append(below_bank)
 
+        centred_banks = {}
+
+        def centre_x(j):
+            for r in range(CENTRED_FOLDS):
+                centred_bank = centred.tile([P, groups_per_tile, P], F32, name="centred_bank")
+                for k in range(groups_per_tile):
+                    nc.tensor.matmul(
+                        out=centred_bank[:, k, :],
+                        lhsT=x_run_sb[:, j * groups_per_tile + k, :],
+                        rhs=turn_x_scaled[:],
+                        start=True,
+                        stop=False,
+                    )
+                    nc.tensor.matmul(
+                        out=centred_bank[:, k, :],
+                        lhsT=below_runs[j][:, r, k, :],
+                        rhs=turn_mask_doubled[:],
+                        start=False,
+                        stop=True,
+                    )
+                centred_banks[j, r] = centred_bank
+
         turn_x(0)
-        make_masks(0)
-        turn_x(1)
-        make_masks(1)
+        for j in range(3):
+            make_masks(j)
         turn_masks(0)
 
         x_codes = keep.tile([P, ROW_TILES * P], U32, align_bytes=64)
@@ -176,8 +202,8 @@ def tile_kanlayer_kernel(tc, x, base_weight_words, base_weight_scales, spline_we
                     )
             return wt
 
-        def take_unit(copy, wt, w_grouped):
-            copy(out=w_grouped[:].rearrange("p e o t -> p (e o t)"), in_=wt[:].rearrange("p e k c -> p (e k c)"))
+        def take_unit(wt, w_grouped):
+            nc.scalar.copy(out=w_grouped[:].rearrange("p e o t -> p (e o t)"), in_=wt[:].rearrange("p e k c -> p (e k c)"))
 
         def quantise_unit(unit, w_grouped):
             c, w = divmod(unit, SPLINE_PAIRS)
@@ -193,20 +219,31 @@ def tile_kanlayer_kernel(tc, x, base_weight_words, base_weight_scales, spline_we
             outer_sq = work.tile([P, FOLDS, TILE_COLS], F32)
             nearest = work.tile([P, 2, TILE_COLS], F32)
             inner_sq = work.tile([P, 2, TILE_COLS], F32)
-            return half_s, outer_sq, nearest, inner_sq
+            shifted = work.tile([P, 2, TILE_COLS], F32)
+            return half_s, outer_sq, nearest, inner_sq, shifted
 
         def scalar_stage(j, cols, tiles, copies):
-            half_s, outer_sq, nearest, inner_sq = tiles
+            half_s, outer_sq, nearest, inner_sq, shifted = tiles
             x_tile = x_banks[j].rearrange("p k c -> p (k c)")[:, cols]
-            for r in range(FOLDS):
+            pairs = (slice(0, 2), slice(2, 4))
+            centred_folds = CENTRED_FOLDS if (j, 0) in centred_banks else 0
+            for r in range(centred_folds, FOLDS):
                 nc.scalar.activation(
                     out=half_s[:, r, cols], in_=x_tile, func=ACT.Abs, scale=1.25, bias=(1.5 - r) / 2.0
                 )
-            pairs = (slice(0, 2), slice(2, 4))
-            for pair in pairs:
+            for r in range(centred_folds):
                 nc.scalar.activation(
-                    out=half_s[:, pair, cols], in_=half_s[:, pair, cols], func=ACT.Abs, scale=1.0, bias=-1.0
+                    out=half_s[:, r, cols],
+                    in_=centred_banks[j, r][:].rearrange("p k c -> p (k c)")[:, cols],
+                    func=ACT.Abs,
+                    scale=1.0,
+                    bias=(3.5 - r) / 2.0 - 2.0,
                 )
+            for pair in pairs:
+                if pair.start >= centred_folds:
+                    nc.scalar.activation(
+                        out=half_s[:, pair, cols], in_=half_s[:, pair, cols], func=ACT.Abs, scale=1.0, bias=-1.0
+                    )
                 if copies:
                     copies.pop(0)()
 
@@ -225,6 +262,10 @@ def tile_kanlayer_kernel(tc, x, base_weight_words, base_weight_scales, spline_we
             )
             if copies:
                 copies.pop(0)()
+            if j in SHIFTED_BY_SCALAR:
+                nc.scalar.activation(
+                    out=shifted[:, :, cols], in_=nearest[:, :, cols], func=ACT.Identity, scale=0.5, bias=ROOT
+                )
             square_outer(pairs[1])
             nc.scalar.activation(
                 out=inner_sq[:, :, cols], in_=nearest[:, :, cols], func=ACT.Square, scale=1.0, bias=-(1.0 + ROOT)
@@ -276,21 +317,25 @@ def tile_kanlayer_kernel(tc, x, base_weight_words, base_weight_scales, spline_we
             nc.scalar.copy(out=result[:], in_=acc[:])
             nc.sync.dma_start(out=out_rows[:, j, :], in_=result[:])
 
-        def multiply_last(j):
-            halves = [slice(0, OUTS // 2), slice(OUTS // 2, OUTS)]
-            accs = []
-            for outs in halves:
+        def open_last(j):
+            halves = []
+            for first_out in range(0, OUTS, OUTS // 2):
+                outs = slice(first_out, first_out + OUTS // 2)
                 acc = banks.tile([P, OUTS], F32, tag="bank", name="acc")
                 x_pass(acc, outs, j)
-                spline_passes(acc, outs, j, range(FOLDS))
-                accs.append(acc)
+                halves.append((acc, outs))
+            return halves
+
+        def finish_last(j, halves):
+            for splines in (range(FOLDS), range(FOLDS, SPLINES)):
+                for acc, outs in halves:
+                    spline_passes(acc, outs, j, splines)
             result = results.tile([P, OUTS], F32, name="result")
-            for acc, outs in zip(accs, halves):
-                spline_passes(acc, outs, j, range(FOLDS, SPLINES))
-            nc.vector.tensor_copy(out=result[:, halves[0]], in_=accs[0][:, halves[0]])
-            nc.sync.dma_start(out=out_rows[:, j, halves[0]], in_=result[:, halves[0]])
-            nc.scalar.copy(out=result[:, halves[1]], in_=accs[1][:, halves[1]])
-            nc.scalar.dma_start(out=out_rows[:, j, halves[1]], in_=result[:, halves[1]])
+            (acc_0, outs_0), (acc_1, outs_1) = halves
+            nc.vector.tensor_copy(out=result[:, outs_0], in_=acc_0[:, outs_0])
+            nc.sync.dma_start(out=out_rows[:, j, outs_0], in_=result[:, outs_0])
+            nc.scalar.copy(out=result[:, outs_1], in_=acc_1[:, outs_1])
+            nc.scalar.dma_start(out=out_rows[:, j, outs_1], in_=result[:, outs_1])
 
         pieces = []
         for j in range(ROW_TILES):
@@ -308,27 +353,22 @@ def tile_kanlayer_kernel(tc, x, base_weight_words, base_weight_scales, spline_we
         accs = []
         staged = []
         scalar_tile(0, [])
+        turn_x(1)
+        centre_x(1)
         for n in range(len(pieces)):
             j, cols, first, last = pieces[n]
-            half_s, outer_sq, nearest, inner_sq = scalar_out[j]
+            half_s, outer_sq, nearest, inner_sq, shifted = scalar_out[j]
             if first:
-                if j + 2 < ROW_TILES:
-                    turn_x(j + 2)
                 next_unit = FIRST_UNITS + j * UNITS_PER_ROW_TILE
                 units = range(next_unit - UNITS_PER_ROW_TILE if j else 0, next_unit) if j <= WEIGHTS_DONE else range(0)
                 copies = []
-                vector_copies = []
                 done_units = staged
                 staged = []
                 for unit in units:
                     w_grouped = weight_stage.tile([P, 2, P, PACK], BF16, align_bytes=64, name="w_grouped")
-                    if unit in VECTOR_UNITS:
-                        vector_copies.append(functools.partial(take_unit, nc.vector.tensor_copy, turn_unit(unit), w_grouped))
-                    else:
-                        copies.append(functools.partial(take_unit, nc.scalar.copy, turn_unit(unit), w_grouped))
+                    copies.append(functools.partial(take_unit, turn_unit(unit), w_grouped))
                     staged.append((unit, w_grouped))
                 minus_outer = scratch.tile([P, FOLDS, TILE_COLS], BF16)
-                shifted = scratch.tile([P, 2, TILE_COLS], F32)
                 inner = scratch.tile([P, 2, TILE_COLS], BF16)
                 outer = scratch.tile([P, FOLDS, TILE_COLS], BF16)
                 value = scratch.tile([P, FOLDS, TILE_COLS], BF16)
@@ -345,12 +385,16 @@ def tile_kanlayer_kernel(tc, x, base_weight_words, base_weight_scales, spline_we
                     accs = [(row_tile, multiply(row_tile)) for row_tile in (3, 4)]
                 if j + 1 < ROW_TILES:
                     scalar_tile(j + 1, copies)
+                if j + 2 < ROW_TILES:
+                    turn_x(j + 2)
+                    centre_x(j + 2)
 
-            for ahead in MASKS_BEFORE.get(n, ()):
-                make_masks(ahead)
-            for copy in vector_copies:
-                copy()
-            vector_copies = []
+            if n == len(pieces) - 1:
+                for row_tile, acc in accs:
+                    store(row_tile, acc)
+                halves = open_last(j)
+            if first and j + 3 < ROW_TILES:
+                make_masks(j + 3)
             pairs = (slice(0, 2), slice(2, 4))
             for pair in pairs:
                 nc.vector.scalar_tensor_tensor(
@@ -361,7 +405,7 @@ def tile_kanlayer_kernel(tc, x, base_weight_words, base_weight_scales, spline_we
                     op0=ALU.subtract,
                     op1=ALU.mult,
                 )
-                if pair.start == 0:
+                if pair.start == 0 and j not in SHIFTED_BY_SCALAR:
                     nc.vector.tensor_scalar(
                         out=shifted[:, :, cols],
                         in0=nearest[:, :, cols],
@@ -406,15 +450,17 @@ def tile_kanlayer_kernel(tc, x, base_weight_words, base_weight_scales, spline_we
                     in1=below_bank[:].rearrange("p e k c -> p e (k c)")[:, :, cols],
                     op=ALU.mult,
                 )
-            for pair in pairs:
-                nc.vector.tensor_tensor(
-                    out=high[:, pair, cols], in0=value[:, pair, cols], in1=low[:, pair, cols], op=ALU.subtract
-                )
             if last:
                 b_codes = codes.tile([P, SPLINES, P], U32, align_bytes=64)
                 b_scales = codes.tile([P, SPLINES, P], U8, align_bytes=64)
                 basis_codes[j] = (b_codes, b_scales)
-                quantise_splines(low, b_codes, b_scales, 0)
+            for pair in pairs:
+                nc.vector.tensor_tensor(
+                    out=high[:, pair, cols], in0=value[:, pair, cols], in1=low[:, pair, cols], op=ALU.subtract
+                )
+                if last and pair.start == (0 if j == ROW_TILES - 1 else 2):
+                    quantise_splines(low, b_codes, b_scales, 0)
+            if last:
                 quantise_splines(high, b_codes, b_scales, FOLDS)
                 if j == ROW_TILES - 2:
                     turn_masks(j + 1)
@@ -422,6 +468,4 @@ def tile_kanlayer_kernel(tc, x, base_weight_words, base_weight_scales, spline_we
                         store(row_tile, acc)
                     accs = [(row_tile, multiply(row_tile)) for row_tile in (5, 6)]
 
-        for row_tile, acc in accs:
-            store(row_tile, acc)
-        multiply_last(ROW_TILES - 1)
+        finish_last(ROW_TILES - 1, halves)

@@ -27,12 +27,13 @@ TILE_COLS = P * PACK
 SPLINE_PAIRS = SPLINES // 2
 WEIGHT_UNITS = OUT_TILES * SPLINE_PAIRS
 GROUP = P // PACK
-UNITS_PER_ROW_TILE = 3
-FIRST_UNITS = 4
+UNITS_IN_TILE = (4, 3, 3, 3, 3)
+UNITS_AHEAD = 2
+X_ROWS_IN_TILE = {4: (0,), 5: (1, 2, 3)}
 MASK_BUFS = 4
 WEIGHTS_DONE = 4
 CENTRED_FOLDS = 2
-SHIFTED_BY_SCALAR = range(WEIGHTS_DONE + 1, ROW_TILES)
+SHIFTED_BY_SCALAR = range(WEIGHTS_DONE + 2, ROW_TILES)
 ROOT = (2.0 ** (1.0 / 3.0) + 2.0 ** (-1.0 / 3.0) - 1.0) / 3.0
 REST = 4.0 * (ROOT * ROOT + ROOT) - (1.0 + ROOT) ** 2
 
@@ -43,7 +44,7 @@ def tile_kanlayer_kernel(tc, x, base_weight_words, base_weight_scales, spline_we
     nc = tc.nc
     with ExitStack() as ctx:
         keep = ctx.enter_context(tc.tile_pool(name="keep", bufs=1))
-        weight_stage = ctx.enter_context(tc.tile_pool(name="weight_stage", bufs=FIRST_UNITS + UNITS_PER_ROW_TILE))
+        weight_stage = ctx.enter_context(tc.tile_pool(name="weight_stage", bufs=8))
         work = ctx.enter_context(tc.tile_pool(name="work", bufs=2))
         scratch = ctx.enter_context(tc.tile_pool(name="scratch", bufs=1))
         codes = ctx.enter_context(tc.tile_pool(name="codes", bufs=WEIGHTS_DONE + 2))
@@ -289,8 +290,8 @@ def tile_kanlayer_kernel(tc, x, base_weight_words, base_weight_scales, spline_we
                 lhsT_scale=x_scales[:, j * P : (j + 1) * P],
                 rhs=base_codes[:, outs].bitcast(FP8X4),
                 rhs_scale=base_scales[:, outs],
-                start=True,
-                stop=False,
+                start=False,
+                stop=True,
             )
 
         def spline_passes(acc, outs, j, splines):
@@ -302,14 +303,18 @@ def tile_kanlayer_kernel(tc, x, base_weight_words, base_weight_scales, spline_we
                     lhsT_scale=b_scales[:, l, :],
                     rhs=w_codes[:, l, outs].bitcast(FP8X4),
                     rhs_scale=w_scales[:, l, outs],
-                    start=False,
-                    stop=(l == SPLINES - 1),
+                    start=(l == 0),
+                    stop=False,
                 )
 
-        def multiply(j):
+        def start_product(j):
             acc = banks.tile([P, OUTS], F32, tag="bank", name="acc")
-            x_pass(acc, slice(0, OUTS), j)
             spline_passes(acc, slice(0, OUTS), j, range(SPLINES))
+            return acc
+
+        def multiply(j):
+            acc = start_product(j)
+            x_pass(acc, slice(0, OUTS), j)
             return acc
 
         def store(j, acc):
@@ -317,19 +322,16 @@ def tile_kanlayer_kernel(tc, x, base_weight_words, base_weight_scales, spline_we
             nc.scalar.copy(out=result[:], in_=acc[:])
             nc.sync.dma_start(out=out_rows[:, j, :], in_=result[:])
 
-        def open_last(j):
+        def multiply_last(j):
             halves = []
             for first_out in range(0, OUTS, OUTS // 2):
-                outs = slice(first_out, first_out + OUTS // 2)
                 acc = banks.tile([P, OUTS], F32, tag="bank", name="acc")
+                halves.append((acc, slice(first_out, first_out + OUTS // 2)))
+            for acc, outs in halves:
+                spline_passes(acc, outs, j, range(FOLDS))
+            for acc, outs in halves:
+                spline_passes(acc, outs, j, range(FOLDS, SPLINES))
                 x_pass(acc, outs, j)
-                halves.append((acc, outs))
-            return halves
-
-        def finish_last(j, halves):
-            for splines in (range(FOLDS), range(FOLDS, SPLINES)):
-                for acc, outs in halves:
-                    spline_passes(acc, outs, j, splines)
             result = results.tile([P, OUTS], F32, name="result")
             (acc_0, outs_0), (acc_1, outs_1) = halves
             nc.vector.tensor_copy(out=result[:, outs_0], in_=acc_0[:, outs_0])
@@ -349,35 +351,43 @@ def tile_kanlayer_kernel(tc, x, base_weight_words, base_weight_scales, spline_we
             for j, cols, first, last in pieces:
                 if j == tile:
                     scalar_stage(j, cols, scalar_out[j], copies)
+            for copy in copies:
+                copy()
 
         accs = []
         staged = []
         scalar_tile(0, [])
+        unit_copies = []
+        unit_tiles = []
+
+        def turn_units(count):
+            for unit in range(len(unit_tiles), len(unit_tiles) + count):
+                w_grouped = weight_stage.tile([P, 2, P, PACK], BF16, align_bytes=64, name="w_grouped")
+                unit_copies.append(functools.partial(take_unit, turn_unit(unit), w_grouped))
+                unit_tiles.append(w_grouped)
+
+        turn_units(UNITS_AHEAD)
         turn_x(1)
         centre_x(1)
         for n in range(len(pieces)):
             j, cols, first, last = pieces[n]
             half_s, outer_sq, nearest, inner_sq, shifted = scalar_out[j]
             if first:
-                next_unit = FIRST_UNITS + j * UNITS_PER_ROW_TILE
-                units = range(next_unit - UNITS_PER_ROW_TILE if j else 0, next_unit) if j <= WEIGHTS_DONE else range(0)
-                copies = []
+                if 0 < j < ROW_TILES - 1:
+                    turn_masks(j)
+                if j < len(UNITS_IN_TILE):
+                    turn_units(sum(UNITS_IN_TILE[: j + 1]) - len(unit_tiles))
                 done_units = staged
-                staged = []
-                for unit in units:
-                    w_grouped = weight_stage.tile([P, 2, P, PACK], BF16, align_bytes=64, name="w_grouped")
-                    copies.append(functools.partial(take_unit, turn_unit(unit), w_grouped))
-                    staged.append((unit, w_grouped))
+                staged = [(unit, unit_tiles[unit]) for unit in range(sum(UNITS_IN_TILE[:j]), sum(UNITS_IN_TILE[: j + 1]))]
+                copies = [unit_copies[unit] for unit, w_grouped in staged]
                 minus_outer = scratch.tile([P, FOLDS, TILE_COLS], BF16)
                 inner = scratch.tile([P, 2, TILE_COLS], BF16)
                 outer = scratch.tile([P, FOLDS, TILE_COLS], BF16)
                 value = scratch.tile([P, FOLDS, TILE_COLS], BF16)
                 low = scratch.tile([P, FOLDS, TILE_COLS], BF16, align_bytes=64)
                 high = scratch.tile([P, FOLDS, TILE_COLS], BF16, align_bytes=64)
-                if 1 <= j <= ROW_TILES // 2:
-                    copies.append(functools.partial(take_x_rows, 2 * (j - 1), turn_x_rows(2 * (j - 1))))
-                if 0 < j < ROW_TILES - 1:
-                    turn_masks(j)
+                for k in X_ROWS_IN_TILE.get(j, ()):
+                    copies.append(functools.partial(take_x_rows, 2 * k, turn_x_rows(2 * k)))
                 for row_tile, acc in accs:
                     store(row_tile, acc)
                 accs = []
@@ -392,7 +402,6 @@ def tile_kanlayer_kernel(tc, x, base_weight_words, base_weight_scales, spline_we
             if n == len(pieces) - 1:
                 for row_tile, acc in accs:
                     store(row_tile, acc)
-                halves = open_last(j)
             if first and j + 3 < ROW_TILES:
                 make_masks(j + 3)
             pairs = (slice(0, 2), slice(2, 4))
@@ -436,9 +445,7 @@ def tile_kanlayer_kernel(tc, x, base_weight_words, base_weight_scales, spline_we
                 for unit, w_grouped in done_units:
                     quantise_unit(unit, w_grouped)
                 if j == WEIGHTS_DONE + 1:
-                    quantise_x()
-                    for multiplied in range(3):
-                        accs.append((multiplied, multiply(multiplied)))
+                    accs = [(row_tile, start_product(row_tile)) for row_tile in range(3)]
             for pair in pairs:
                 nc.vector.tensor_tensor(
                     out=value[:, pair, cols], in0=outer[:, pair, cols], in1=inner[:, :, cols], op=ALU.min
@@ -462,10 +469,14 @@ def tile_kanlayer_kernel(tc, x, base_weight_words, base_weight_scales, spline_we
                     quantise_splines(low, b_codes, b_scales, 0)
             if last:
                 quantise_splines(high, b_codes, b_scales, FOLDS)
+                if j == WEIGHTS_DONE + 1:
+                    quantise_x()
+                    for row_tile, acc in accs:
+                        x_pass(acc, slice(0, OUTS), row_tile)
                 if j == ROW_TILES - 2:
                     turn_masks(j + 1)
                     for row_tile, acc in accs:
                         store(row_tile, acc)
                     accs = [(row_tile, multiply(row_tile)) for row_tile in (5, 6)]
 
-        finish_last(ROW_TILES - 1, halves)
+        multiply_last(ROW_TILES - 1)

@@ -30,7 +30,6 @@ GROUP = P // PACK
 UNITS_IN_TILE = (4, 3, 3, 3, 3)
 UNITS_AHEAD = 2
 X_ROWS_IN_TILE = {4: (0,), 5: (1, 2, 3)}
-MASK_BUFS = 4
 WEIGHTS_DONE = 4
 CENTRED_FOLDS = 2
 SHIFTED_BY_SCALAR = range(WEIGHTS_DONE + 2, ROW_TILES)
@@ -44,12 +43,11 @@ def tile_kanlayer_kernel(tc, x, base_weight_words, base_weight_scales, spline_we
     nc = tc.nc
     with ExitStack() as ctx:
         keep = ctx.enter_context(tc.tile_pool(name="keep", bufs=1))
-        weight_stage = ctx.enter_context(tc.tile_pool(name="weight_stage", bufs=8))
+        weight_stage = ctx.enter_context(tc.tile_pool(name="weight_stage", bufs=7))
         work = ctx.enter_context(tc.tile_pool(name="work", bufs=2))
         scratch = ctx.enter_context(tc.tile_pool(name="scratch", bufs=1))
         codes = ctx.enter_context(tc.tile_pool(name="codes", bufs=WEIGHTS_DONE + 2))
         results = ctx.enter_context(tc.tile_pool(name="results", bufs=4))
-        mask_stage = ctx.enter_context(tc.tile_pool(name="mask_stage", bufs=MASK_BUFS))
         turned_x = ctx.enter_context(tc.psum_pool(name="turned_x", bufs=1))
         centred = ctx.enter_context(tc.psum_pool(name="centred", bufs=CENTRED_FOLDS))
         turned_masks = ctx.enter_context(tc.psum_pool(name="turned_masks", bufs=2))
@@ -76,7 +74,7 @@ def tile_kanlayer_kernel(tc, x, base_weight_words, base_weight_scales, spline_we
             nc.sync.dma_start(out=x_run_sb[:, groups, :], in_=x_runs[:, groups, :])
 
         w_runs = spline_weight.rearrange("o (t p) l -> (o t) (p l)", t=PACK).rearrange("(g q) f -> q g f", q=P)
-        w_sb = keep.tile([P, OUTS // GROUP, P, SPLINES], BF16)
+        w_sb = keep.tile([P, OUTS // GROUP, P, SPLINES], BF16, align_bytes=64)
 
         def load_w_runs(c):
             groups = slice(c * groups_per_tile, (c + 1) * groups_per_tile)
@@ -91,8 +89,16 @@ def tile_kanlayer_kernel(tc, x, base_weight_words, base_weight_scales, spline_we
         load_x_runs(4, ROW_TILES - 4)
         for c in range(1, OUT_TILES):
             load_w_runs(c)
-        x_sb = keep.tile([P, ROW_TILES, FEATURES], BF16)
-        nc.sync.dma_start(out=x_sb[:], in_=x.rearrange("(j p) i -> p j i", p=P))
+        x_sb = w_sb[:, :groups_per_tile, :, :].rearrange("q g p l -> q (g p l)").rearrange("q (j i) -> q j i", i=FEATURES)
+        x_grouped = (
+            w_sb[:, groups_per_tile : 2 * groups_per_tile, :, :]
+            .rearrange("q g p l -> q (g p l)")
+            .rearrange("q (j b t) -> q j b t", b=P, t=PACK)
+        )
+
+        def load_x_rows():
+            nc.sync.dma_start(out=x_sb, in_=x.rearrange("(j p) i -> p j i", p=P))
+
         out_rows = out.rearrange("(j p) o -> p j o", p=P)
         base_codes = keep.tile([P, OUTS], U32, align_bytes=64)
         nc.sync.dma_start(
@@ -105,9 +111,6 @@ def tile_kanlayer_kernel(tc, x, base_weight_words, base_weight_scales, spline_we
                 in_=base_weight_scales[0, 4 * quadrant : 4 * quadrant + 4, :].bitcast(I32),
             )
 
-        def groups_of(j):
-            return slice(j * groups_per_tile, (j + 1) * groups_per_tile)
-
         x_banks = {}
 
         def turn_x(j):
@@ -116,15 +119,15 @@ def tile_kanlayer_kernel(tc, x, base_weight_words, base_weight_scales, spline_we
             for k in range(groups_per_tile):
                 nc.tensor.transpose(x_bank[:, 0, k, :], x_run_sb[:, j * groups_per_tile + k, :], ident_bf16[:])
 
-        below_runs = {}
+        below_run_sb = keep.tile([P, FOLDS, BATCH // GROUP, P], BF16)
         below_banks = {}
 
-        def make_masks(j):
-            below_runs[j] = mask_stage.tile([P, FOLDS, groups_per_tile, P], BF16, name="below_run")
+        def make_masks(first, count):
+            groups = slice(first * groups_per_tile, (first + count) * groups_per_tile)
             for r in range(FOLDS):
                 nc.vector.tensor_scalar(
-                    out=below_runs[j][:, r, :, :],
-                    in0=x_run_sb[:, groups_of(j), :],
+                    out=below_run_sb[:, r, groups, :],
+                    in0=x_run_sb[:, groups, :],
                     scalar1=(r - 1.5) / 2.5,
                     scalar2=None,
                     op0=ALU.is_lt,
@@ -136,7 +139,11 @@ def tile_kanlayer_kernel(tc, x, base_weight_words, base_weight_scales, spline_we
                 below_bank = turned_masks.tile([P, 2, groups_per_tile, P], BF16, name="below_bank")
                 for e in range(2):
                     for k in range(groups_per_tile):
-                        nc.tensor.transpose(below_bank[:, e, k, :], below_runs[j][:, first_fold + e, k, :], ident_bf16[:])
+                        nc.tensor.transpose(
+                            below_bank[:, e, k, :],
+                            below_run_sb[:, first_fold + e, j * groups_per_tile + k, :],
+                            ident_bf16[:],
+                        )
                 below_banks[j].append(below_bank)
 
         centred_banks = {}
@@ -154,7 +161,7 @@ def tile_kanlayer_kernel(tc, x, base_weight_words, base_weight_scales, spline_we
                     )
                     nc.tensor.matmul(
                         out=centred_bank[:, k, :],
-                        lhsT=below_runs[j][:, r, k, :],
+                        lhsT=below_run_sb[:, r, j * groups_per_tile + k, :],
                         rhs=turn_mask_doubled[:],
                         start=False,
                         stop=True,
@@ -162,16 +169,16 @@ def tile_kanlayer_kernel(tc, x, base_weight_words, base_weight_scales, spline_we
                 centred_banks[j, r] = centred_bank
 
         turn_x(0)
-        for j in range(3):
-            make_masks(j)
+        make_masks(0, 1)
+        make_masks(1, 1)
+        make_masks(2, 2)
         turn_masks(0)
 
         x_codes = keep.tile([P, ROW_TILES * P], U32, align_bytes=64)
         x_scales = keep.tile([P, ROW_TILES * P], U8, align_bytes=64)
-        x_grouped = keep.tile([P, ROW_TILES, P, PACK], BF16, align_bytes=64)
 
         def turn_x_rows(j):
-            x_words = x_sb[:].bitcast(F32)
+            x_words = x_sb.bitcast(F32)
             xt = banks.tile([P, 2, 2, P], F32, tag="bank", name="xt")
             for k in range(2):
                 for u in range(2):
@@ -180,14 +187,14 @@ def tile_kanlayer_kernel(tc, x, base_weight_words, base_weight_scales, spline_we
 
         def take_x_rows(j, xt):
             nc.scalar.copy(
-                out=x_grouped[:].bitcast(F32)[:, j : j + 2, :, :], in_=xt[:].rearrange("p k u b -> p k b u")
+                out=x_grouped.bitcast(F32)[:, j : j + 2, :, :], in_=xt[:].rearrange("p k u b -> p k b u")
             )
 
         def quantise_x():
             nc.vector.quantize_mx(
                 out=x_codes[:].bitcast(FP8X4),
                 scales=x_scales[:],
-                in_=x_grouped[:].rearrange("p j b t -> p (j b t)"),
+                in_=x_grouped.rearrange("p j b t -> p (j b t)"),
             )
 
         w_codes = keep.tile([P, SPLINES, OUTS], U32, align_bytes=64)
@@ -274,27 +281,29 @@ def tile_kanlayer_kernel(tc, x, base_weight_words, base_weight_scales, spline_we
             if copies:
                 copies.pop(0)()
 
-        def quantise_splines(four_splines, b_codes, b_scales, l0):
-            nc.vector.quantize_mx(
-                out=b_codes[:, l0 : l0 + FOLDS, :].rearrange("p l b -> p (l b)").bitcast(FP8X4),
-                scales=b_scales[:, l0 : l0 + FOLDS, :].rearrange("p l b -> p (l b)"),
-                in_=four_splines[:].rearrange("p r c -> p (r c)"),
-            )
-
         basis_codes = {}
 
-        def x_pass(acc, outs, j):
+        def quantise_splines(four_splines, folds, j, l0):
+            b_codes, b_scales = basis_codes[j]
+            splines = slice(l0 + folds.start, l0 + folds.stop)
+            nc.vector.quantize_mx(
+                out=b_codes[:, splines, :].rearrange("p l b -> p (l b)").bitcast(FP8X4),
+                scales=b_scales[:, splines, :].rearrange("p l b -> p (l b)"),
+                in_=four_splines[:, folds, :].rearrange("p r c -> p (r c)"),
+            )
+
+        def x_pass(acc, outs, j, start, stop):
             nc.tensor.matmul_mx(
                 out=acc[:, outs],
                 lhsT=x_codes[:, j * P : (j + 1) * P].bitcast(FP8X4),
                 lhsT_scale=x_scales[:, j * P : (j + 1) * P],
                 rhs=base_codes[:, outs].bitcast(FP8X4),
                 rhs_scale=base_scales[:, outs],
-                start=False,
-                stop=True,
+                start=start,
+                stop=stop,
             )
 
-        def spline_passes(acc, outs, j, splines):
+        def spline_passes(acc, outs, j, splines, start, stop):
             b_codes, b_scales = basis_codes[j]
             for l in splines:
                 nc.tensor.matmul_mx(
@@ -303,18 +312,18 @@ def tile_kanlayer_kernel(tc, x, base_weight_words, base_weight_scales, spline_we
                     lhsT_scale=b_scales[:, l, :],
                     rhs=w_codes[:, l, outs].bitcast(FP8X4),
                     rhs_scale=w_scales[:, l, outs],
-                    start=(l == 0),
-                    stop=False,
+                    start=(start and l == splines[0]),
+                    stop=(stop and l == splines[-1]),
                 )
 
         def start_product(j):
             acc = banks.tile([P, OUTS], F32, tag="bank", name="acc")
-            spline_passes(acc, slice(0, OUTS), j, range(SPLINES))
+            spline_passes(acc, slice(0, OUTS), j, range(SPLINES), start=True, stop=False)
             return acc
 
         def multiply(j):
             acc = start_product(j)
-            x_pass(acc, slice(0, OUTS), j)
+            x_pass(acc, slice(0, OUTS), j, start=False, stop=True)
             return acc
 
         def store(j, acc):
@@ -325,13 +334,13 @@ def tile_kanlayer_kernel(tc, x, base_weight_words, base_weight_scales, spline_we
         def multiply_last(j):
             halves = []
             for first_out in range(0, OUTS, OUTS // 2):
+                outs = slice(first_out, first_out + OUTS // 2)
                 acc = banks.tile([P, OUTS], F32, tag="bank", name="acc")
-                halves.append((acc, slice(first_out, first_out + OUTS // 2)))
-            for acc, outs in halves:
-                spline_passes(acc, outs, j, range(FOLDS))
-            for acc, outs in halves:
-                spline_passes(acc, outs, j, range(FOLDS, SPLINES))
-                x_pass(acc, outs, j)
+                x_pass(acc, outs, j, start=True, stop=False)
+                halves.append((acc, outs))
+            for l in range(0, SPLINES, 2):
+                for acc, outs in halves:
+                    spline_passes(acc, outs, j, range(l, l + 2), start=False, stop=(l + 2 == SPLINES))
             result = results.tile([P, OUTS], F32, name="result")
             (acc_0, outs_0), (acc_1, outs_1) = halves
             nc.vector.tensor_copy(out=result[:, outs_0], in_=acc_0[:, outs_0])
@@ -375,6 +384,8 @@ def tile_kanlayer_kernel(tc, x, base_weight_words, base_weight_scales, spline_we
             if first:
                 if 0 < j < ROW_TILES - 1:
                     turn_masks(j)
+                if j == 1:
+                    load_x_rows()
                 if j < len(UNITS_IN_TILE):
                     turn_units(sum(UNITS_IN_TILE[: j + 1]) - len(unit_tiles))
                 done_units = staged
@@ -402,8 +413,8 @@ def tile_kanlayer_kernel(tc, x, base_weight_words, base_weight_scales, spline_we
             if n == len(pieces) - 1:
                 for row_tile, acc in accs:
                     store(row_tile, acc)
-            if first and j + 3 < ROW_TILES:
-                make_masks(j + 3)
+            if first and j == 1:
+                make_masks(4, ROW_TILES - 4)
             pairs = (slice(0, 2), slice(2, 4))
             for pair in pairs:
                 nc.vector.scalar_tensor_tensor(
@@ -461,18 +472,24 @@ def tile_kanlayer_kernel(tc, x, base_weight_words, base_weight_scales, spline_we
                 b_codes = codes.tile([P, SPLINES, P], U32, align_bytes=64)
                 b_scales = codes.tile([P, SPLINES, P], U8, align_bytes=64)
                 basis_codes[j] = (b_codes, b_scales)
+            in_pairs = last and j == ROW_TILES - 1
             for pair in pairs:
+                if in_pairs:
+                    quantise_splines(low, pair, j, 0)
                 nc.vector.tensor_tensor(
                     out=high[:, pair, cols], in0=value[:, pair, cols], in1=low[:, pair, cols], op=ALU.subtract
                 )
-                if last and pair.start == (0 if j == ROW_TILES - 1 else 2):
-                    quantise_splines(low, b_codes, b_scales, 0)
             if last:
-                quantise_splines(high, b_codes, b_scales, FOLDS)
+                if in_pairs:
+                    for pair in pairs:
+                        quantise_splines(high, pair, j, FOLDS)
+                else:
+                    quantise_splines(low, slice(0, FOLDS), j, 0)
+                    quantise_splines(high, slice(0, FOLDS), j, FOLDS)
                 if j == WEIGHTS_DONE + 1:
                     quantise_x()
                     for row_tile, acc in accs:
-                        x_pass(acc, slice(0, OUTS), row_tile)
+                        x_pass(acc, slice(0, OUTS), row_tile, start=False, stop=True)
                 if j == ROW_TILES - 2:
                     turn_masks(j + 1)
                     for row_tile, acc in accs:

@@ -69,8 +69,8 @@ def tile_kanlayer_kernel(tc, x, base_weight_words, base_weight_scales, spline_we
         x_run_sb = keep.tile([P, BATCH // GROUP, P], BF16)
         groups_per_tile = P // GROUP
 
-        def load_x_runs(first, count):
-            groups = slice(first * groups_per_tile, (first + count) * groups_per_tile)
+        def load_x_runs(first_group, count):
+            groups = slice(first_group, first_group + count)
             nc.sync.dma_start(out=x_run_sb[:, groups, :], in_=x_runs[:, groups, :])
 
         w_runs = spline_weight.rearrange("o (t p) l -> (o t) (p l)", t=PACK).rearrange("(g q) f -> q g f", q=P)
@@ -82,11 +82,12 @@ def tile_kanlayer_kernel(tc, x, base_weight_words, base_weight_scales, spline_we
                 out=w_sb[:, groups, :, :].rearrange("q g p l -> q g (p l)"), in_=w_runs[:, groups, :]
             )
 
-        load_x_runs(0, 1)
-        load_x_runs(1, 1)
-        load_x_runs(2, 2)
+        load_x_runs(0, groups_per_tile // 2)
+        load_x_runs(groups_per_tile // 2, groups_per_tile // 2)
+        load_x_runs(groups_per_tile, groups_per_tile)
+        load_x_runs(2 * groups_per_tile, 2 * groups_per_tile)
         load_w_runs(0)
-        load_x_runs(4, ROW_TILES - 4)
+        load_x_runs(4 * groups_per_tile, (ROW_TILES - 4) * groups_per_tile)
         for c in range(1, OUT_TILES):
             load_w_runs(c)
         x_sb = w_sb[:, :groups_per_tile, :, :].rearrange("q g p l -> q (g p l)").rearrange("q (j i) -> q j i", i=FEATURES)
@@ -270,11 +271,11 @@ def tile_kanlayer_kernel(tc, x, base_weight_words, base_weight_scales, spline_we
             )
             if copies:
                 copies.pop(0)()
+            square_outer(pairs[1])
             if j in SHIFTED_BY_SCALAR:
                 nc.scalar.activation(
                     out=shifted[:, :, cols], in_=nearest[:, :, cols], func=ACT.Identity, scale=0.5, bias=ROOT
                 )
-            square_outer(pairs[1])
             nc.scalar.activation(
                 out=inner_sq[:, :, cols], in_=nearest[:, :, cols], func=ACT.Square, scale=1.0, bias=-(1.0 + ROOT)
             )

import functools
import math
from contextlib import ExitStack

import concourse.mybir as mybir
from concourse.masks import make_identity

F32 = mybir.dt.float32
BF16 = mybir.dt.bfloat16
I32 = mybir.dt.int32
U32 = mybir.dt.uint32
U8 = mybir.dt.uint8
FP8X4 = mybir.dt.float8_e4m3fn_x4
ACT = mybir.ActivationFunctionType
ALU = mybir.AluOpType

P = 128
PACK = 4
BATCH = 1024
FEATURES = P * PACK
OUTS = 512
SPLINES = 8
FOLDS = SPLINES // 2
ROW_TILES = BATCH // P
OUT_TILES = OUTS // P
TILE_COLS = P * PACK
SPLINE_PAIRS = SPLINES // 2
WEIGHT_UNITS = OUT_TILES * SPLINE_PAIRS
GROUP = P // PACK
UNITS_IN_TILE = (4, 3, 3, 3, 3)
UNITS_AHEAD = 2
X_ROWS_IN_TILE = {4: (0,), 5: (1, 2, 3)}
WEIGHTS_DONE = 4
CENTRED_FOLDS = 2
SHIFTED_BY_SCALAR = range(WEIGHTS_DONE + 2, ROW_TILES)
ROOT = (2.0 ** (1.0 / 3.0) + 2.0 ** (-1.0 / 3.0) - 1.0) / 3.0
REST = 4.0 * (ROOT * ROOT + ROOT) - (1.0 + ROOT) ** 2

FLOPS = 2 * BATCH * OUTS * (FEATURES + FEATURES * SPLINES)


def tile_kanlayer_kernel(tc, x, base_weight_words, base_weight_scales, spline_weight, out):
    nc = tc.nc
    with ExitStack() as ctx:
        keep = ctx.enter_context(tc.tile_pool(name="keep", bufs=1))
        weight_stage = ctx.enter_context(tc.tile_pool(name="weight_stage", bufs=7))
        work = ctx.enter_context(tc.tile_pool(name="work", bufs=2))
        scratch = ctx.enter_context(tc.tile_pool(name="scratch", bufs=1))
        codes = ctx.enter_context(tc.tile_pool(name="codes", bufs=WEIGHTS_DONE + 2))
        results = ctx.enter_context(tc.tile_pool(name="results", bufs=4))
        turned_x = ctx.enter_context(tc.psum_pool(name="turned_x", bufs=1))
        centred = ctx.enter_context(tc.psum_pool(name="centred", bufs=CENTRED_FOLDS))
        turned_masks = ctx.enter_context(tc.psum_pool(name="turned_masks", bufs=2))
        banks = ctx.enter_context(tc.psum_pool(name="banks", bufs=3))
        ctx.enter_context(tc.manual_schedule())

        ident = keep.tile([P, P], F32)
        make_identity(nc, ident[:])
        ident_bf16 = keep.tile([P, P], BF16)
        make_identity(nc, ident_bf16[:])
        turn_x_scaled = keep.tile([P, P], BF16)
        nc.scalar.activation(out=turn_x_scaled[:], in_=ident_bf16[:], func=ACT.Copy, scale=1.25)
        turn_mask_doubled = keep.tile([P, P], BF16)
        nc.scalar.activation(out=turn_mask_doubled[:], in_=ident_bf16[:], func=ACT.Copy, scale=2.0)
        base_scales = keep.tile([P, OUTS], U8, align_bytes=64)
        nc.vector.memset(base_scales[:].bitcast(I32), 0)

        x_runs = x.rearrange("b (t p) -> (b t) p", t=PACK).rearrange("(g q) p -> q g p", q=P)
        x_run_sb = keep.tile([P, BATCH // GROUP, P], BF16)
        groups_per_tile = P // GROUP

        def load_x_runs(first_group, count):
            groups = slice(first_group, first_group + count)
            nc.sync.dma_start(out=x_run_sb[:, groups, :], in_=x_runs[:, groups, :])

        w_runs = spline_weight.rearrange("o (t p) l -> (o t) (p l)", t=PACK).rearrange("(g q) f -> q g f", q=P)
        w_sb = keep.tile([P, OUTS // GROUP, P, SPLINES], BF16, align_bytes=64)

        def load_w_runs(c):
            groups = slice(c * groups_per_tile, (c + 1) * groups_per_tile)
            nc.sync.dma_start(
                out=w_sb[:, groups, :, :].rearrange("q g p l -> q g (p l)"), in_=w_runs[:, groups, :]
            )

        load_x_runs(0, groups_per_tile // 2)
        load_x_runs(groups_per_tile // 2, groups_per_tile // 2)
        load_x_runs(groups_per_tile, groups_per_tile)
        load_x_runs(2 * groups_per_tile, 2 * groups_per_tile)
        load_w_runs(0)
        load_x_runs(4 * groups_per_tile, (ROW_TILES - 4) * groups_per_tile)
        for c in range(1, OUT_TILES):
            load_w_runs(c)
        x_sb = w_sb[:, :groups_per_tile, :, :].rearrange("q g p l -> q (g p l)").rearrange("q (j i) -> q j i", i=FEATURES)
        x_grouped = (
            w_sb[:, groups_per_tile : 2 * groups_per_tile, :, :]
            .rearrange("q g p l -> q (g p l)")
            .rearrange("q (j b t) -> q j b t", b=P, t=PACK)
        )

        def load_x_rows():
            nc.sync.dma_start(out=x_sb, in_=x.rearrange("(j p) i -> p j i", p=P))

        out_rows = out.rearrange("(j p) o -> p j o", p=P)
        base_codes = keep.tile([P, OUTS], U32, align_bytes=64)
        nc.sync.dma_start(
            out=base_codes[:].bitcast(I32),
            in_=base_weight_words[0].rearrange("p n t -> p (n t)").bitcast(I32),
        )
        for quadrant in range(4):
            nc.sync.dma_start(
                out=base_scales[32 * quadrant : 32 * quadrant + 4, :].bitcast(I32),
                in_=base_weight_scales[0, 4 * quadrant : 4 * quadrant + 4, :].bitcast(I32),
            )

        x_banks = {}

        def turn_x(j):
            x_bank = turned_x.tile([P, 2, groups_per_tile, P], BF16, name="x_bank")
            x_banks[j] = x_bank[:, 0, :, :]
            for k in range(groups_per_tile):
                nc.tensor.transpose(x_bank[:, 0, k, :], x_run_sb[:, j * groups_per_tile + k, :], ident_bf16[:])

        below_run_sb = keep.tile([P, FOLDS, BATCH // GROUP, P], BF16)
        below_banks = {}

        def make_masks(first, count):
            groups = slice(first * groups_per_tile, (first + count) * groups_per_tile)
            for r in range(FOLDS):
                nc.vector.tensor_scalar(
                    out=below_run_sb[:, r, groups, :],
                    in0=x_run_sb[:, groups, :],
                    scalar1=(r - 1.5) / 2.5,
                    scalar2=None,
                    op0=ALU.is_lt,
                )

        def turn_masks(j):
            below_banks[j] = []
            for first_fold in range(0, FOLDS, 2):
                below_bank = turned_masks.tile([P, 2, groups_per_tile, P], BF16, name="below_bank")
                for e in range(2):
                    for k in range(groups_per_tile):
                        nc.tensor.transpose(
                            below_bank[:, e, k, :],
                            below_run_sb[:, first_fold + e, j * groups_per_tile + k, :],
                            ident_bf16[:],
                        )
                below_banks[j].append(below_bank)

        centred_banks = {}

        def centre_x(j):
            for r in range(CENTRED_FOLDS):
                centred_bank = centred.tile([P, groups_per_tile, P], F32, name="centred_bank")
                for k in range(groups_per_tile):
                    nc.tensor.matmul(
                        out=centred_bank[:, k, :],
                        lhsT=x_run_sb[:, j * groups_per_tile + k, :],
                        rhs=turn_x_scaled[:],
                        start=True,
                        stop=False,
                    )
                    nc.tensor.matmul(
                        out=centred_bank[:, k, :],
                        lhsT=below_run_sb[:, r, j * groups_per_tile + k, :],
                        rhs=turn_mask_doubled[:],
                        start=False,
                        stop=True,
                    )
                centred_banks[j, r] = centred_bank

        turn_x(0)
        make_masks(0, 1)
        make_masks(1, 1)
        make_masks(2, 2)
        turn_masks(0)

        x_codes = keep.tile([P, ROW_TILES * P], U32, align_bytes=64)
        x_scales = keep.tile([P, ROW_TILES * P], U8, align_bytes=64)

        def turn_x_rows(j):
            x_words = x_sb.bitcast(F32)
            xt = banks.tile([P, 2, 2, P], F32, tag="bank", name="xt")
            for k in range(2):
                for u in range(2):
                    nc.tensor.transpose(xt[:, k, u, :], x_words[:, j + k, u : FEATURES // 2 : 2], ident[:])
            return xt

        def take_x_rows(j, xt):
            nc.scalar.copy(
                out=x_grouped.bitcast(F32)[:, j : j + 2, :, :], in_=xt[:].rearrange("p k u b -> p k b u")
            )

        def quantise_x():
            nc.vector.quantize_mx(
                out=x_codes[:].bitcast(FP8X4),
                scales=x_scales[:],
                in_=x_grouped.rearrange("p j b t -> p (j b t)"),
            )

        w_codes = keep.tile([P, SPLINES, OUTS], U32, align_bytes=64)
        w_scales = keep.tile([P, SPLINES, OUTS], U8, align_bytes=64)

        def turn_unit(unit):
            c, w = divmod(unit, SPLINE_PAIRS)
            wt = banks.tile([P, 2, groups_per_tile, P], BF16, tag="bank", name="wt")
            for e in range(2):
                for k in range(groups_per_tile):
                    nc.tensor.transpose(
                        wt[:, e, k, :], w_sb[:, c * groups_per_tile + k, :, 2 * w + e], ident_bf16[:]
                    )
            return wt

        def take_unit(wt, w_grouped):
            nc.scalar.copy(out=w_grouped[:].rearrange("p e o t -> p (e o t)"), in_=wt[:].rearrange("p e k c -> p (e k c)"))

        def quantise_unit(unit, w_grouped):
            c, w = divmod(unit, SPLINE_PAIRS)
            for e in range(2):
                nc.vector.quantize_mx(
                    out=w_codes[:, 2 * w + e, c * P : (c + 1) * P].bitcast(FP8X4),
                    scales=w_scales[:, 2 * w + e, c * P : (c + 1) * P],
                    in_=w_grouped[:, e, :, :].rearrange("p o t -> p (o t)"),
                )

        def scalar_tiles():
            half_s = work.tile([P, FOLDS, TILE_COLS], F32)
            outer_sq = work.tile([P, FOLDS, TILE_COLS], F32)
            nearest = work.tile([P, 2, TILE_COLS], F32)
            inner_sq = work.tile([P, 2, TILE_COLS], F32)
            shifted = work.tile([P, 2, TILE_COLS], F32)
            return half_s, outer_sq, nearest, inner_sq, shifted

        def scalar_stage(j, cols, tiles, copies):
            half_s, outer_sq, nearest, inner_sq, shifted = tiles
            x_tile = x_banks[j].rearrange("p k c -> p (k c)")[:, cols]
            pairs = (slice(0, 2), slice(2, 4))
            centred_folds = CENTRED_FOLDS if (j, 0) in centred_banks else 0
            for r in range(centred_folds, FOLDS):
                nc.scalar.activation(
                    out=half_s[:, r, cols], in_=x_tile, func=ACT.Abs, scale=1.25, bias=(1.5 - r) / 2.0
                )
            for r in range(centred_folds):
                nc.scalar.activation(
                    out=half_s[:, r, cols],
                    in_=centred_banks[j, r][:].rearrange("p k c -> p (k c)")[:, cols],
                    func=ACT.Abs,
                    scale=1.0,
                    bias=(3.5 - r) / 2.0 - 2.0,
                )
            for pair in pairs:
                if pair.start >= centred_folds:
                    nc.scalar.activation(
                        out=half_s[:, pair, cols], in_=half_s[:, pair, cols], func=ACT.Abs, scale=1.0, bias=-1.0
                    )
                if copies:
                    copies.pop(0)()

            def square_outer(pair):
                nc.scalar.activation(
                    out=outer_sq[:, pair, cols],
                    in_=half_s[:, pair, cols],
                    func=ACT.Square,
                    scale=math.sqrt(4.0 / 3.0),
                    bias=-math.sqrt(4.0 / 3.0),
                )

            square_outer(pairs[0])
            nc.scalar.activation(
                out=nearest[:, :, cols], in_=half_s[:, 1:3, cols], func=ACT.Abs, scale=2.0, bias=-1.0
            )
            if copies:
                copies.pop(0)()
            square_outer(pairs[1])
            if j in SHIFTED_BY_SCALAR:
                nc.scalar.activation(
                    out=shifted[:, :, cols], in_=nearest[:, :, cols], func=ACT.Identity, scale=0.5, bias=ROOT
                )
            nc.scalar.activation(
                out=inner_sq[:, :, cols], in_=nearest[:, :, cols], func=ACT.Square, scale=1.0, bias=-(1.0 + ROOT)
            )
            if copies:
                copies.pop(0)()

        basis_codes = {}

        def quantise_splines(four_splines, folds, j, l0):
            b_codes, b_scales = basis_codes[j]
            splines = slice(l0 + folds.start, l0 + folds.stop)
            nc.vector.quantize_mx(
                out=b_codes[:, splines, :].rearrange("p l b -> p (l b)").bitcast(FP8X4),
                scales=b_scales[:, splines, :].rearrange("p l b -> p (l b)"),
                in_=four_splines[:, folds, :].rearrange("p r c -> p (r c)"),
            )

        def x_pass(acc, outs, j, start, stop):
            nc.tensor.matmul_mx(
                out=acc[:, outs],
                lhsT=x_codes[:, j * P : (j + 1) * P].bitcast(FP8X4),
                lhsT_scale=x_scales[:, j * P : (j + 1) * P],
                rhs=base_codes[:, outs].bitcast(FP8X4),
                rhs_scale=base_scales[:, outs],
                start=start,
                stop=stop,
            )

        def spline_passes(acc, outs, j, splines, start, stop):
            b_codes, b_scales = basis_codes[j]
            for l in splines:
                nc.tensor.matmul_mx(
                    out=acc[:, outs],
                    lhsT=b_codes[:, l, :].bitcast(FP8X4),
                    lhsT_scale=b_scales[:, l, :],
                    rhs=w_codes[:, l, outs].bitcast(FP8X4),
                    rhs_scale=w_scales[:, l, outs],
                    start=(start and l == splines[0]),
                    stop=(stop and l == splines[-1]),
                )

        def start_product(j):
            acc = banks.tile([P, OUTS], F32, tag="bank", name="acc")
            spline_passes(acc, slice(0, OUTS), j, range(SPLINES), start=True, stop=False)
            return acc

        def multiply(j):
            acc = start_product(j)
            x_pass(acc, slice(0, OUTS), j, start=False, stop=True)
            return acc

        def store(j, acc):
            result = results.tile([P, OUTS], F32, name="result")
            nc.scalar.copy(out=result[:], in_=acc[:])
            nc.sync.dma_start(out=out_rows[:, j, :], in_=result[:])

        def multiply_last(j):
            halves = []
            for first_out in range(0, OUTS, OUTS // 2):
                outs = slice(first_out, first_out + OUTS // 2)
                acc = banks.tile([P, OUTS], F32, tag="bank", name="acc")
                x_pass(acc, outs, j, start=True, stop=False)
                halves.append((acc, outs))
            for l in range(0, SPLINES, 2):
                for acc, outs in halves:
                    spline_passes(acc, outs, j, range(l, l + 2), start=False, stop=(l + 2 == SPLINES))
            result = results.tile([P, OUTS], F32, name="result")
            (acc_0, outs_0), (acc_1, outs_1) = halves
            nc.vector.tensor_copy(out=result[:, outs_0], in_=acc_0[:, outs_0])
            nc.sync.dma_start(out=out_rows[:, j, outs_0], in_=result[:, outs_0])
            nc.scalar.copy(out=result[:, outs_1], in_=acc_1[:, outs_1])
            nc.scalar.dma_start(out=out_rows[:, j, outs_1], in_=result[:, outs_1])

        pieces = []
        for j in range(ROW_TILES):
            cuts = [0, TILE_COLS // 2, TILE_COLS] if j in (0, ROW_TILES - 1) else [0, TILE_COLS]
            for k in range(len(cuts) - 1):
                pieces.append((j, slice(cuts[k], cuts[k + 1]), k == 0, k == len(cuts) - 2))
        scalar_out = {}

        def scalar_tile(tile, copies):
            scalar_out[tile] = scalar_tiles()
            for j, cols, first, last in pieces:
                if j == tile:
                    scalar_stage(j, cols, scalar_out[j], copies)
            for copy in copies:
                copy()

        accs = []
        staged = []
        scalar_tile(0, [])
        unit_copies = []
        unit_tiles = []

        def turn_units(count):
            for unit in range(len(unit_tiles), len(unit_tiles) + count):
                w_grouped = weight_stage.tile([P, 2, P, PACK], BF16, align_bytes=64, name="w_grouped")
                unit_copies.append(functools.partial(take_unit, turn_unit(unit), w_grouped))
                unit_tiles.append(w_grouped)

        turn_units(UNITS_AHEAD)
        turn_x(1)
        centre_x(1)
        for n in range(len(pieces)):
            j, cols, first, last = pieces[n]
            half_s, outer_sq, nearest, inner_sq, shifted = scalar_out[j]
            if first:
                if 0 < j < ROW_TILES - 1:
                    turn_masks(j)
                if j == 1:
                    load_x_rows()
                if j < len(UNITS_IN_TILE):
                    turn_units(sum(UNITS_IN_TILE[: j + 1]) - len(unit_tiles))
                done_units = staged
                staged = [(unit, unit_tiles[unit]) for unit in range(sum(UNITS_IN_TILE[:j]), sum(UNITS_IN_TILE[: j + 1]))]
                copies = [unit_copies[unit] for unit, w_grouped in staged]
                minus_outer = scratch.tile([P, FOLDS, TILE_COLS], BF16)
                inner = scratch.tile([P, 2, TILE_COLS], BF16)
                outer = scratch.tile([P, FOLDS, TILE_COLS], BF16)
                value = scratch.tile([P, FOLDS, TILE_COLS], BF16)
                low = scratch.tile([P, FOLDS, TILE_COLS], BF16, align_bytes=64)
                high = scratch.tile([P, FOLDS, TILE_COLS], BF16, align_bytes=64)
                for k in X_ROWS_IN_TILE.get(j, ()):
                    copies.append(functools.partial(take_x_rows, 2 * k, turn_x_rows(2 * k)))
                for row_tile, acc in accs:
                    store(row_tile, acc)
                accs = []
                if j == ROW_TILES - 2:
                    accs = [(row_tile, multiply(row_tile)) for row_tile in (3, 4)]
                if j + 1 < ROW_TILES:
                    scalar_tile(j + 1, copies)
                if j + 2 < ROW_TILES:
                    turn_x(j + 2)
                    centre_x(j + 2)

            if n == len(pieces) - 1:
                for row_tile, acc in accs:
                    store(row_tile, acc)
            if first and j == 1:
                make_masks(4, ROW_TILES - 4)
            pairs = (slice(0, 2), slice(2, 4))
            for pair in pairs:
                nc.vector.scalar_tensor_tensor(
                    out=minus_outer[:, pair, cols],
                    in0=half_s[:, pair, cols],
                    scalar=1.0,
                    in1=outer_sq[:, pair, cols],
                    op0=ALU.subtract,
                    op1=ALU.mult,
                )
                if pair.start == 0 and j not in SHIFTED_BY_SCALAR:
                    nc.vector.tensor_scalar(
                        out=shifted[:, :, cols],
                        in0=nearest[:, :, cols],
                        scalar1=0.5,
                        scalar2=ROOT,
                        op0=ALU.mult,
                        op1=ALU.add,
                    )
            for pair in pairs:
                nc.vector.tensor_scalar(
                    out=outer[:, pair, cols],
                    in0=minus_outer[:, pair, cols],
                    scalar1=-1.0,
                    scalar2=0.0,
                    op0=ALU.mult,
                    op1=ALU.max,
                )
                if pair.start == 0:
                    nc.vector.scalar_tensor_tensor(
                        out=inner[:, :, cols],
                        in0=inner_sq[:, :, cols],
                        scalar=REST,
                        in1=shifted[:, :, cols],
                        op0=ALU.add,
                        op1=ALU.mult,
                    )
            if first:
                for unit, w_grouped in done_units:
                    quantise_unit(unit, w_grouped)
                if j == WEIGHTS_DONE + 1:
                    accs = [(row_tile, start_product(row_tile)) for row_tile in range(3)]
            for pair in pairs:
                nc.vector.tensor_tensor(
                    out=value[:, pair, cols], in0=outer[:, pair, cols], in1=inner[:, :, cols], op=ALU.min
                )
            for pair, below_bank in zip(pairs, below_banks[j]):
                nc.vector.tensor_tensor(
                    out=low[:, pair, cols],
                    in0=value[:, pair, cols],
                    in1=below_bank[:].rearrange("p e k c -> p e (k c)")[:, :, cols],
                    op=ALU.mult,
                )
            if last:
                b_codes = codes.tile([P, SPLINES, P], U32, align_bytes=64)
                b_scales = codes.tile([P, SPLINES, P], U8, align_bytes=64)
                basis_codes[j] = (b_codes, b_scales)
            in_pairs = last and j == ROW_TILES - 1
            for pair in pairs:
                if in_pairs:
                    quantise_splines(low, pair, j, 0)
                nc.vector.tensor_tensor(
                    out=high[:, pair, cols], in0=value[:, pair, cols], in1=low[:, pair, cols], op=ALU.subtract
                )
            if last:
                if in_pairs:
                    for pair in pairs:
                        quantise_splines(high, pair, j, FOLDS)
                else:
                    quantise_splines(low, slice(0, FOLDS), j, 0)
                    quantise_splines(high, slice(0, FOLDS), j, FOLDS)
                if j == WEIGHTS_DONE + 1:
                    quantise_x()
                    for row_tile, acc in accs:
                        x_pass(acc, slice(0, OUTS), row_tile, start=False, stop=True)
                if j == ROW_TILES - 2:
                    turn_masks(j + 1)
                    for row_tile, acc in accs:
                        store(row_tile, acc)
                    accs = [(row_tile, multiply(row_tile)) for row_tile in (5, 6)]

        multiply_last(ROW_TILES - 1)
